import numpy as np
import ml_dtypes


def mxq(x, axis, fmt="e4m3"):
    dtype, down = {"e4m3": (ml_dtypes.float8_e4m3fn, 7), "e5m2": (ml_dtypes.float8_e5m2, 14)}[fmt]
    v = np.moveaxis(np.asarray(x, np.float32).astype(ml_dtypes.bfloat16).astype(np.float64), axis, -1)
    blocks = v.reshape(v.shape[:-1] + (-1, 32))
    amax = np.abs(blocks).max(-1, keepdims=True)
    byte = np.maximum(np.where(amax > 0, np.frexp(amax)[1] - 1 + 127, 0) - down, 1)
    scale = np.exp2(byte - 127.0)
    codes = (blocks / scale).astype(np.float32).astype(dtype).astype(np.float64)
    return np.moveaxis((codes * scale).reshape(v.shape), -1, axis)


WIDE = False


def mx_kscale(k):
    if not WIDE:
        return np.ones(k)
    levels = np.array([18, -18])
    if k % 512:
        return np.exp2(np.random.permutation(np.resize(levels, k // 32))).repeat(32)
    a = np.empty((k // 512, 16))
    for p in range(k // 512):
        a[p, :8] = np.random.permutation(np.resize(levels, 8))
        for g in range(8):
            far = levels[np.abs(levels - a[p, g]) >= 10]
            a[p, g + 8] = far[np.random.randint(len(far))]
    return np.exp2(a.ravel()).repeat(32)


BF16 = ml_dtypes.bfloat16


def bf(x):
    return np.asarray(x, np.float32).astype(BF16)


def f64(x):
    return np.asarray(x).astype(np.float64)


B, C, CQ, CV, H, W = 32, 1024, 256, 1024, 4, 8
P = H * W
T = B * P
J = CQ + CQ + CV


def tokens(y):
    return y.transpose(0, 2, 3, 1).reshape(T, y.shape[1])


def unpool(g):
    return g[:, :, :H, None] / W + g[:, :, None, H:] / H


def draw_grad(o, s, u):
    e = np.exp2(np.random.randint(-6, 1, (B, 1, H + W)))
    return bf(np.random.standard_normal((B, o, H + W)) * e * 4.0 / s[:, None, None] * u[None, :, None])


def setup_inputs():
    s = mx_kscale(T)[::P]
    u = mx_kscale(J)
    uq, uk, uv = u[:CQ], u[CQ:2 * CQ], u[2 * CQ:]
    c = 3.0 / np.sqrt(C)
    x = bf(np.random.standard_normal((B, C, H, W)) * s[:, None, None, None])
    Wq = bf(np.random.standard_normal((CQ, C)) * c / uq[:, None])
    bq = bf(np.random.standard_normal(CQ) * 0.1)
    Wk = bf(np.random.standard_normal((CQ, C)) * c / uk[:, None])
    bk = bf(np.random.standard_normal(CQ) * 0.1)
    Wv = bf(np.random.standard_normal((CV, C)) * c / uv[:, None])
    bv = bf(np.random.standard_normal(CV) * 0.1)
    g0 = draw_grad(CQ, s, uq)
    g1 = draw_grad(CQ, s, uk)
    g2 = draw_grad(CV, s, uv)
    return {"x": x, "Wq": Wq, "bq": bq, "Wk": Wk, "bk": bk, "Wv": Wv, "bv": bv,
            "grad_0": g0, "grad_1": g1, "grad_2": g2}


def reference(x, Wq, bq, Wk, bk, Wv, bv, grad_0, grad_1, grad_2):
    dz = np.concatenate([tokens(unpool(f64(grad_0))), tokens(unpool(f64(grad_1))), tokens(unpool(f64(grad_2)))], axis=1)
    w = np.concatenate([f64(Wq), f64(Wk), f64(Wv)], axis=0)
    dx = mxq(dz, 1, "e5m2") @ mxq(w, 0, "e4m3")
    xq = mxq(tokens(f64(x)), 0, "e4m3")
    dw = mxq(dz, 0, "e5m2").T @ xq
    dx = dx.reshape(B, H, W, C).transpose(0, 3, 1, 2)
    return dx, dw[:CQ], dw[CQ:2 * CQ], dw[2 * CQ:]

@@ -1,0 +1,275 @@
+from contextlib import ExitStack
+
+import concourse.mybir as mybir
+from concourse.masks import make_identity
+
+F32 = mybir.dt.float32
+BF16 = mybir.dt.bfloat16
+U32 = mybir.dt.uint32
+U8 = mybir.dt.uint8
+E4M3 = mybir.dt.float8_e4m3fn_x4
+E5M2 = mybir.dt.float8_e5m2_x4
+COPY = mybir.ActivationFunctionType.Copy
+ADD = mybir.AluOpType.add
+
+P = 128
+T, C, J = 1024, 1024, 1536
+NG = 3
+FLOPS = 2 * 2 * T * C * J
+BYTES = 2 * (T * C + J * C + 32 * J * 12) + 4 * (T * C + J * C)
+
+PLAN = """
+gTp:v:1 wc:v:1,1 wc:v:1,0 gTp:v:4 gTp:v:2 qw:v:1,0 gTp:v:3 qw:v:1,1 gTe:a:1 gTe:a:2 gTe:v:4 wc:v:0,1 gTp:v:5
+gTe:a:3 gTe:v:5 gTp:v:0 gTe:a:0 add:v:2,0 add:v:0,0 add:v:1,0 xs:v:0 qw:v:0,1 wc:a:2,0 qf:v:0,0 dTp:v:0,0,1
+dTp:v:2,0,0 dTp:v:0,0,0 wc:a:2,1 qf:v:1,0 dTp:v:2,0,1 xTp:v:0,0 dTe:a:0,0,0 xTp:v:0,3 xTp:v:0,2 qf:v:2,0
+dxm:v:0,7,0 dxm:v:0,5,0 qw:v:2,1 xTe:a:0,2 wc:v:0,0 qw:v:0,0 xTe:a:0,0 dxm:v:0,6,0 qw:v:2,0 dxm:v:0,6,1
+dxm:v:0,4,0 dxm:v:0,7,1 dxm:v:0,4,1 dTe:a:2,0,0 dTe:a:2,0,1 dxm:v:0,6,2 dxm:v:0,7,2 dxm:v:0,5,1 xTp:v:0,1
+dxm:v:0,5,2 dxo:a:0,6 dxm:v:0,4,2 xTe:a:0,1 dxm:v:0,0,0 dxm:v:0,2,0 dxo:a:0,4 dxm:v:0,3,0 xTe:v:0,3 xs:v:1
+dTe:a:0,0,1 dxo:a:0,7 add:v:0,1 dxm:v:0,0,1 qx:v:0 dxm:v:0,1,0 dxm:v:0,0,2 dxm:v:0,2,1 dxm:v:0,3,1 dxm:v:0,1,1
+dxo:a:0,0 dxo:a:0,5 dxm:v:0,3,2 add:v:1,1 dxm:v:0,1,2 dxo:a:0,3 dxm:v:0,2,2 dxo:a:0,1 xTp:v:1,1 dTp:v:1,0,0
+dTp:v:0,1,1 xTp:v:1,2 dTe:a:1,0,0 dTp:v:0,1,0 qf:v:0,1 xTp:v:1,3 dxo:v:0,2 dTp:v:1,1,0 xTe:a:1,2 xTe:a:1,1
+dTp:v:1,0,1 xTp:v:1,0 dTp:v:1,1,1 dxm:v:1,3,0 xTe:a:1,3 xTe:a:1,0 dTe:a:1,0,1 qf:v:1,1 dxm:v:1,5,0 dxm:v:1,4,0
+dxm:v:1,3,1 add:v:2,1 sdx:v:0,1 dxm:v:1,5,1 qf:v:2,1 dxm:v:1,4,1 dxm:v:1,3,2 dxm:v:1,1,0 dxo:a:1,3 qt:v:0,0
+dxm:v:1,5,2 dxm:v:1,1,1 dxm:v:1,7,0 qt:v:1,0 dxo:v:1,5 sdx:v:0,0 dTe:v:0,1,0 dxm:v:1,1,2 dxm:v:1,4,2
+dTe:a:0,1,1 dxm:v:1,2,0 dxm:v:1,7,1 dxo:a:1,4 dxm:v:1,6,0 dxm:v:1,2,1 qx:v:1 dxm:v:1,0,0 dxm:v:1,2,2
+dxm:v:1,0,1 dxm:v:1,7,2 dxo:a:1,1 sdx:v:0,3 qt:v:0,1 dxm:v:1,6,1 sdx:v:0,2 dxo:a:1,2 dxm:v:1,0,2 dxo:v:1,0
+dxm:v:1,6,2 dxo:a:1,7 dTp:v:2,1,1 dTe:v:1,1,1 dwm:v:0,1,0 dxo:a:1,6 dwm:v:3,0,0 dwm:v:1,0,0 dwm:v:2,0,0
+qt:v:2,0 dwm:v:1,0,1 dwm:v:1,1,0 dwm:v:1,1,1 dTp:v:2,1,0 dTe:a:1,1,0 dwo:a:1,1 qt:v:1,1 dwo:v:1,0 dwm:v:2,0,1
+dwm:v:9,0,0 sdx:v:1,0 dwm:v:2,1,0 dwm:v:0,1,1 dTe:v:2,1,1 dwm:v:2,1,1 dwo:a:2,0 dwm:v:9,1,0 dwm:v:8,0,0
+dwo:v:2,1 dwm:v:3,1,0 dwm:v:0,0,0 sdx:v:1,2 dTe:a:2,1,0 dwm:v:5,1,0 qt:v:2,1 dwm:v:3,1,1 dwm:v:9,0,1 sdx:v:1,3
+sdw:v:1 dwm:v:0,0,1 dwm:v:9,1,1 dwo:v:0,0 dwm:v:5,1,1 dwm:v:3,0,1 sdw:v:2 dwo:v:3,0 dwo:a:0,1 dwm:v:8,0,1
+dwo:a:9,1 dwo:a:8,0 dwm:v:5,0,0 dwm:v:5,0,1 dwm:v:10,0,0 dwm:v:10,1,0 dwo:v:3,1 dwm:v:7,1,0 dwo:a:9,0
+dwo:a:5,1 sdx:v:1,1 dwm:v:10,0,1 sdw:v:0 sdw:v:9 dwm:v:7,1,1 dwm:v:6,1,0 dwm:v:10,1,1 dwm:v:6,0,0 dwm:v:6,1,1
+dwo:v:5,0 dwo:v:7,1 dwm:v:8,1,0 dwm:v:4,1,0 dwm:v:11,0,0 dwm:v:11,0,1 dwm:v:7,0,0 dwo:a:10,0 sdw:v:3
+dwo:v:10,1 dwm:v:8,1,1 dwm:v:6,0,1 dwo:v:6,0 dwm:v:4,0,0 dwo:a:6,1 sdw:v:5 dwo:a:11,0 dwm:v:4,1,1 dwm:v:11,1,0
+sdw:v:10 dwm:v:7,0,1 dwm:v:4,0,1 dwo:v:4,1 dwo:v:4,0 dwo:v:7,0 sdw:v:6 dwm:v:11,1,1 dwo:v:11,1 dwo:a:8,1
+sdw:v:8 sdw:v:4 sdw:v:7 sdw:v:11
+"""
+LOADS = "w1 g w0 w2 x0 x1"
+
+
+def tile_pam_module_pa_v_kernel(
+    tc, x, Wq, bq, Wk, bk, Wv, bv, grad_0, grad_1, grad_2, out_0, out_1, out_2, out_3
+):
+    nc = tc.nc
+    with ExitStack() as ctx:
+        keep = ctx.enter_context(tc.tile_pool(name="keep", bufs=1))
+        work = ctx.enter_context(tc.tile_pool(name="work", bufs=2))
+        psum = ctx.enter_context(tc.psum_pool(name="psum", bufs=8))
+        ctx.enter_context(tc.manual_schedule())
+
+        gnat = keep.tile([P, 6144], BF16, name="gnat", align_bytes=64)
+        w_raw = [keep.tile([P, 4, C], BF16, name="w_raw%d" % g, align_bytes=64) for g in range(NG)]
+        x_raw = [keep.tile([P, 16, 256], BF16, name="x_raw%d" % h, align_bytes=64) for h in range(2)]
+        ident = keep.tile([P, P], F32, name="ident")
+        make_identity(nc, ident[:])
+        nc.vector.memset(gnat[96:128, :], 0.0)
+
+        def load(name):
+            i = int(name[1]) if len(name) > 1 else 0
+            if name == "g":
+                nc.sync.dma_start(out=gnat[0:32, 0:3072], in_=grad_0.rearrange("n f v -> n (f v)"))
+                nc.scalar.dma_start(out=gnat[32:64, :], in_=grad_2[:, 0:512, :].rearrange("n f v -> n (f v)"))
+                nc.sync.dma_start(out=gnat[0:32, 3072:6144], in_=grad_1.rearrange("n f v -> n (f v)"))
+                nc.scalar.dma_start(out=gnat[64:96, :], in_=grad_2[:, 512:1024, :].rearrange("n f v -> n (f v)"))
+            elif name == "w0":
+                nc.sync.dma_start(out=w_raw[0][0:64], in_=Wq.rearrange("(p j) c -> p j c", j=4))
+                nc.sync.dma_start(out=w_raw[0][64:128], in_=Wk.rearrange("(p j) c -> p j c", j=4))
+            elif name[0] == "w":
+                nc.sync.dma_start(
+                    out=w_raw[i][:], in_=Wv[512 * i - 512 : 512 * i, :].rearrange("(p j) c -> p j c", j=4)
+                )
+            else:
+                nc.sync.dma_start(
+                    out=x_raw[i][:], in_=x[16 * i : 16 * i + 16].rearrange("n (p e) i j -> p n (e i j)", e=8)
+                )
+
+        for name in LOADS.split():
+            load(name)
+
+        g_row = keep.tile([P, 2, 96, 2, 4], BF16, name="g_row", align_bytes=64)
+        g_col = keep.tile([P, 96, 8, 4], BF16, name="g_col", align_bytes=64)
+        w_codes = keep.tile([P, NG, C], U32, name="w_codes", align_bytes=64)
+        w_scales = keep.tile([P, NG, C], U8, name="w_scales", align_bytes=64)
+        f_codes = keep.tile([P, NG, T], U32, name="f_codes", align_bytes=64)
+        f_scales = keep.tile([P, NG, T], U8, name="f_scales", align_bytes=64)
+        t_codes = keep.tile([P, 2, J], U32, name="t_codes", align_bytes=64)
+        t_scales = keep.tile([P, 2, J], U8, name="t_scales", align_bytes=64)
+        x_codes = keep.tile([P, 2, C], U32, name="x_codes", align_bytes=64)
+        x_scales = keep.tile([P, 2, C], U8, name="x_scales", align_bytes=64)
+        tiles = {}
+
+        def bank(key, shape):
+            b = psum.tile(shape, F32, name="bank", tag="bank", bufs=8)
+            tiles[key] = b
+            return b
+
+        def stage(key, tag, bufs):
+            t = work.tile([P, 4096 if tag[0] == "x" else 2048], BF16, name=tag, tag=tag, bufs=bufs, align_bytes=64)
+            tiles[key] = t
+            return t
+
+        def move(engine, out, in_):
+            if engine == "a":
+                nc.scalar.copy(out=out, in_=in_)
+            else:
+                nc.vector.tensor_copy(out=out, in_=in_)
+
+        g_words = gnat[:].bitcast(F32).rearrange("q (m t w) -> q t w m", t=4, w=6)
+
+        def gTp(en, w):
+            pg = bank(("g", w), [P, 4, P])
+            for t in range(4):
+                nc.tensor.transpose(pg[:, t, :], g_words[:, t, w, :], ident[:])
+
+        def gTe(en, w):
+            src = tiles["g", w][:].rearrange("p t q -> p (t q)").bitcast(BF16)
+            src = src.rearrange("p (t q e) -> p q e t", t=4, e=2)[:, 0:96]
+            if w < 2:
+                out, factor = g_row[:, w], 0.125
+            else:
+                out, factor = g_col[:, :, 2 * (w - 2) : 2 * (w - 2) + 2, :], 0.25
+            if en == "a":
+                nc.scalar.activation(out=out, in_=src, func=COPY, scale=factor)
+            else:
+                nc.vector.tensor_scalar_mul(out, src, factor)
+
+        def add(en, g, h):
+            dz = stage(("dz", g, h), "dz", 4)
+            q0 = 32 * g + 16 * h
+            shape = [P, 16, 2, 8, 4]
+            for u in range(2):
+                nc.vector.tensor_tensor(
+                    out=dz[:, 1024 * u : 1024 * (u + 1)].rearrange("p (n a j t) -> p n a j t", n=16, a=2, j=8),
+                    in0=g_row[:, u, q0 : q0 + 16].unsqueeze(3).to_broadcast(shape),
+                    in1=g_col[:, q0 : q0 + 16].unsqueeze(2).to_broadcast(shape),
+                    op=ADD,
+                )
+
+        def qf(en, g, h):
+            cols = slice(512 * h, 512 * h + 512)
+            nc.vector.quantize_mx(
+                out=f_codes[:, g, cols].bitcast(E5M2), scales=f_scales[:, g, cols], in_=tiles["dz", g, h][:]
+            )
+
+        def dTp(en, g, h, v):
+            words = tiles["dz", g, h][:].bitcast(F32).rearrange("p (u q e v) -> p u q e v", u=2, e=2, v=2)
+            pt = bank(("d", g, h, v), [P, 4, P])
+            for s in range(4):
+                nc.tensor.transpose(pt[:, s, :], words[:, s // 2, :, s % 2, v], ident[:])
+
+        def dTe(en, g, h, v):
+            if ("tok", g, h) not in tiles:
+                stage(("tok", g, h), "tok", 3)
+            dst = tiles["tok", g, h][:].rearrange("q (p v f s) -> q v p f s", v=2, f=2, s=4)
+            src = tiles["d", g, h, v][:].rearrange("q s p -> q (s p)").bitcast(BF16)
+            move(en, dst[:, v], src.rearrange("q (s p f) -> q p f s", s=4, f=2))
+
+        def qt(en, g, h):
+            cols = slice(512 * g, 512 * g + 512)
+            nc.vector.quantize_mx(
+                out=t_codes[:, h, cols].bitcast(E5M2), scales=t_scales[:, h, cols], in_=tiles["tok", g, h][:]
+            )
+
+        def wc(en, g, k):
+            grouped = stage(("wg", g, k), "wg", 3)
+            move(
+                en,
+                grouped[:].rearrange("p (e m j) -> p e m j", e=4, j=4),
+                w_raw[g][:].rearrange("p j (m e) -> p e m j", e=8)[:, 4 * k : 4 * k + 4],
+            )
+
+        def qw(en, g, k):
+            cols = slice(512 * k, 512 * k + 512)
+            nc.vector.quantize_mx(
+                out=w_codes[:, g, cols].bitcast(E4M3), scales=w_scales[:, g, cols], in_=tiles["wg", g, k][:]
+            )
+
+        def xs(en, h):
+            xr = stage(("xr", h), "xr", 1)
+            nc.vector.tensor_copy(
+                out=xr[:].rearrange("p (b n k) -> p b n k", b=16, n=16),
+                in_=x_raw[h][:].rearrange("p n (b k) -> p b n k", k=16),
+            )
+
+        def xTp(en, h, k):
+            words = tiles["xr", h][:].bitcast(F32).rearrange("p (b q) -> p b q", b=16)
+            px = bank(("x", h, k), [P, 4, P])
+            for s in range(4):
+                nc.tensor.transpose(px[:, s, :], words[:, 4 * k + s, :], ident[:])
+
+        def xTe(en, h, k):
+            if ("xg", h) not in tiles:
+                stage(("xg", h), "xg", 1)
+            dst = tiles["xg", h][:].bitcast(F32).rearrange("q (p s) -> q p s", s=16)[:, :, 4 * k : 4 * k + 4]
+            move(en, dst, tiles["x", h, k][:].rearrange("q s p -> q p s"))
+
+        def qx(en, h):
+            nc.vector.quantize_mx(
+                out=x_codes[:, h, :].bitcast(E4M3), scales=x_scales[:, h, :], in_=tiles["xg", h][:]
+            )
+
+        def dxm(en, h, e, g):
+            acc = bank(("dx", h, e), [P, 512]) if g == 0 else tiles["dx", h, e]
+            wcol = slice(128 * e, 128 * e + 128)
+            tk = slice(512 * h, 512 * h + 512)
+            nc.tensor.matmul_mx(
+                out=acc[:],
+                lhsT=w_codes[:, g, wcol].bitcast(E4M3),
+                lhsT_scale=w_scales[:, g, wcol],
+                rhs=f_codes[:, g, tk].bitcast(E5M2),
+                rhs_scale=f_scales[:, g, tk],
+                start=(g == 0),
+                stop=(g == NG - 1),
+            )
+
+        def dxo(en, h, e):
+            if ("dxt", h) not in tiles:
+                tiles["dxt", h] = work.tile([P, 16, 8, 32], F32, name="dx_out", tag="dx_out", bufs=2)
+            dst = tiles["dxt", h][:, :, e, :].rearrange("m n (u k) -> m n u k", u=2)
+            move(en, dst, tiles["dx", h, e][:].rearrange("m (u n k) -> m n u k", u=2, n=16))
+
+        def sdx(en, h, k):
+            n0 = 16 * h + 4 * k
+            nc.sync.dma_start(
+                out=out_0[n0 : n0 + 4].rearrange("n (m e) i j -> m n (e i j)", e=8),
+                in_=tiles["dxt", h][:, 4 * k : 4 * k + 4].rearrange("m n e t -> m n (e t)"),
+            )
+
+        def dwm(en, oc, b, h):
+            acc = bank(("dw", oc, b), [P, 512]) if h == 0 else tiles["dw", oc, b]
+            fc = slice(128 * oc, 128 * oc + 128)
+            cc = slice(512 * b, 512 * b + 512)
+            nc.tensor.matmul_mx(
+                out=acc[:],
+                lhsT=t_codes[:, h, fc].bitcast(E5M2),
+                lhsT_scale=t_scales[:, h, fc],
+                rhs=x_codes[:, h, cc].bitcast(E4M3),
+                rhs_scale=x_scales[:, h, cc],
+                start=(h == 0),
+                stop=(h == 1),
+            )
+
+        def dwo(en, oc, b):
+            if ("row", oc) not in tiles:
+                tiles["row", oc] = work.tile([P, C], F32, name="dw_out", tag="dw_out", bufs=4)
+            move(en, tiles["row", oc][:, 512 * b : 512 * b + 512], tiles["dw", oc, b][:])
+
+        def sdw(en, oc):
+            fc = slice(128 * oc, 128 * oc + 128)
+            if oc < 2:
+                dst = out_1[fc, :]
+            elif oc < 4:
+                dst = out_2[128 * (oc - 2) : 128 * (oc - 1), :]
+            else:
+                dst = out_3[128 * (oc - 4) : 128 * (oc - 3), :]
+            nc.sync.dma_start(out=dst, in_=tiles["row", oc][:])
+
+        steps = {
+            "gTp": gTp, "gTe": gTe, "add": add, "qf": qf, "dTp": dTp, "dTe": dTe, "qt": qt, "wc": wc, "qw": qw,
+            "xs": xs, "xTp": xTp, "xTe": xTe, "qx": qx, "dxm": dxm, "dxo": dxo, "sdx": sdx, "dwm": dwm, "dwo": dwo,
+            "sdw": sdw,
+        }
+        for step in PLAN.split():
+            name, engine, where = step.split(":")
+            steps[name](engine, *[int(i) for i in where.split(",")])

@@ -19,33 +19,34 @@ FLOPS = 2 * 2 * T * C * J
 BYTES = 2 * (T * C + J * C + 32 * J * 12) + 4 * (T * C + J * C)
 
 PLAN = """
-gTp:v:1 wc:v:1,1 wc:v:1,0 gTp:v:4 gTp:v:2 qw:v:1,0 gTp:v:3 qw:v:1,1 gTe:a:1 gTe:a:2 gTe:v:4 wc:v:0,1 gTp:v:5
-gTe:a:3 gTe:v:5 gTp:v:0 gTe:a:0 add:v:2,0 add:v:0,0 add:v:1,0 xs:v:0 qw:v:0,1 wc:a:2,0 qf:v:0,0 dTp:v:0,0,1
-dTp:v:2,0,0 dTp:v:0,0,0 wc:a:2,1 qf:v:1,0 dTp:v:2,0,1 xTp:v:0,0 dTe:a:0,0,0 xTp:v:0,3 xTp:v:0,2 qf:v:2,0
-dxm:v:0,7,0 dxm:v:0,5,0 qw:v:2,1 xTe:a:0,2 wc:v:0,0 qw:v:0,0 xTe:a:0,0 dxm:v:0,6,0 qw:v:2,0 dxm:v:0,6,1
-dxm:v:0,4,0 dxm:v:0,7,1 dxm:v:0,4,1 dTe:a:2,0,0 dTe:a:2,0,1 dxm:v:0,6,2 dxm:v:0,7,2 dxm:v:0,5,1 xTp:v:0,1
-dxm:v:0,5,2 dxo:a:0,6 dxm:v:0,4,2 xTe:a:0,1 dxm:v:0,0,0 dxm:v:0,2,0 dxo:a:0,4 dxm:v:0,3,0 xTe:v:0,3 xs:v:1
-dTe:a:0,0,1 dxo:a:0,7 add:v:0,1 dxm:v:0,0,1 qx:v:0 dxm:v:0,1,0 dxm:v:0,0,2 dxm:v:0,2,1 dxm:v:0,3,1 dxm:v:0,1,1
-dxo:a:0,0 dxo:a:0,5 dxm:v:0,3,2 add:v:1,1 dxm:v:0,1,2 dxo:a:0,3 dxm:v:0,2,2 dxo:a:0,1 xTp:v:1,1 dTp:v:1,0,0
-dTp:v:0,1,1 xTp:v:1,2 dTe:a:1,0,0 dTp:v:0,1,0 qf:v:0,1 xTp:v:1,3 dxo:v:0,2 dTp:v:1,1,0 xTe:a:1,2 xTe:a:1,1
-dTp:v:1,0,1 xTp:v:1,0 dTp:v:1,1,1 dxm:v:1,3,0 xTe:a:1,3 xTe:a:1,0 dTe:a:1,0,1 qf:v:1,1 dxm:v:1,5,0 dxm:v:1,4,0
-dxm:v:1,3,1 add:v:2,1 sdx:v:0,1 dxm:v:1,5,1 qf:v:2,1 dxm:v:1,4,1 dxm:v:1,3,2 dxm:v:1,1,0 dxo:a:1,3 qt:v:0,0
-dxm:v:1,5,2 dxm:v:1,1,1 dxm:v:1,7,0 qt:v:1,0 dxo:v:1,5 sdx:v:0,0 dTe:v:0,1,0 dxm:v:1,1,2 dxm:v:1,4,2
-dTe:a:0,1,1 dxm:v:1,2,0 dxm:v:1,7,1 dxo:a:1,4 dxm:v:1,6,0 dxm:v:1,2,1 qx:v:1 dxm:v:1,0,0 dxm:v:1,2,2
-dxm:v:1,0,1 dxm:v:1,7,2 dxo:a:1,1 sdx:v:0,3 qt:v:0,1 dxm:v:1,6,1 sdx:v:0,2 dxo:a:1,2 dxm:v:1,0,2 dxo:v:1,0
-dxm:v:1,6,2 dxo:a:1,7 dTp:v:2,1,1 dTe:v:1,1,1 dwm:v:0,1,0 dxo:a:1,6 dwm:v:3,0,0 dwm:v:1,0,0 dwm:v:2,0,0
-qt:v:2,0 dwm:v:1,0,1 dwm:v:1,1,0 dwm:v:1,1,1 dTp:v:2,1,0 dTe:a:1,1,0 dwo:a:1,1 qt:v:1,1 dwo:v:1,0 dwm:v:2,0,1
-dwm:v:9,0,0 sdx:v:1,0 dwm:v:2,1,0 dwm:v:0,1,1 dTe:v:2,1,1 dwm:v:2,1,1 dwo:a:2,0 dwm:v:9,1,0 dwm:v:8,0,0
-dwo:v:2,1 dwm:v:3,1,0 dwm:v:0,0,0 sdx:v:1,2 dTe:a:2,1,0 dwm:v:5,1,0 qt:v:2,1 dwm:v:3,1,1 dwm:v:9,0,1 sdx:v:1,3
-sdw:v:1 dwm:v:0,0,1 dwm:v:9,1,1 dwo:v:0,0 dwm:v:5,1,1 dwm:v:3,0,1 sdw:v:2 dwo:v:3,0 dwo:a:0,1 dwm:v:8,0,1
-dwo:a:9,1 dwo:a:8,0 dwm:v:5,0,0 dwm:v:5,0,1 dwm:v:10,0,0 dwm:v:10,1,0 dwo:v:3,1 dwm:v:7,1,0 dwo:a:9,0
-dwo:a:5,1 sdx:v:1,1 dwm:v:10,0,1 sdw:v:0 sdw:v:9 dwm:v:7,1,1 dwm:v:6,1,0 dwm:v:10,1,1 dwm:v:6,0,0 dwm:v:6,1,1
-dwo:v:5,0 dwo:v:7,1 dwm:v:8,1,0 dwm:v:4,1,0 dwm:v:11,0,0 dwm:v:11,0,1 dwm:v:7,0,0 dwo:a:10,0 sdw:v:3
-dwo:v:10,1 dwm:v:8,1,1 dwm:v:6,0,1 dwo:v:6,0 dwm:v:4,0,0 dwo:a:6,1 sdw:v:5 dwo:a:11,0 dwm:v:4,1,1 dwm:v:11,1,0
-sdw:v:10 dwm:v:7,0,1 dwm:v:4,0,1 dwo:v:4,1 dwo:v:4,0 dwo:v:7,0 sdw:v:6 dwm:v:11,1,1 dwo:v:11,1 dwo:a:8,1
-sdw:v:8 sdw:v:4 sdw:v:7 sdw:v:11
+wc:v:1,0 qw:v:1,0 wc:v:1,1 qw:v:1,1 gTp:v:4 gTe:v:4 gTp:v:2 gTp:v:1 gTe:a:2 gTp:v:3 wc:v:0,1 gTe:a:1 gTp:v:0
+wc:v:0,0 gTe:a:3 xs:v:0 gTe:a:0 gTp:v:5 gTe:a:5 qw:v:0,0 qw:v:0,1 add:v:0,0 xTp:v:0,2 add:v:1,0 qf:v:0,0
+xTe:a:0,2 xTp:v:0,3 xTp:v:0,0 wc:a:2,1 qf:v:1,0 xTe:v:0,3 dTp:v:0,0,0 xTp:v:0,1 dTp:v:1,0,0 dTp:v:1,0,1
+xTe:a:0,1 dTe:a:1,0,0 add:v:2,0 dxm:v:0,1,0 dxm:v:0,6,0 dxm:v:0,2,0 dxm:v:0,7,0 dxm:v:0,7,1 dTe:a:1,0,1
+qw:v:2,1 qf:v:2,0 dxm:v:0,5,0 xTe:v:0,0 wc:a:2,0 dxm:v:0,2,1 dxm:v:0,6,1 add:v:2,1 dxm:v:0,4,0 qw:v:2,0
+dxm:v:0,4,1 dxm:v:0,5,1 dxm:v:0,1,1 dxm:v:0,5,2 xs:v:1 dxm:v:0,6,2 dxo:a:0,5 add:v:0,1 dxm:v:0,4,2 dTp:v:2,0,0
+dxo:a:0,4 dxm:v:0,7,2 dxm:v:0,3,0 dxo:a:0,6 dxm:v:0,1,2 dxm:v:0,3,1 dxm:v:0,3,2 dxo:a:0,7 dxm:v:0,2,2
+dxm:v:0,0,0 dxm:v:0,0,1 dxo:a:0,3 dxo:v:0,2 dxm:v:0,0,2 dxo:a:0,1 dTp:v:2,1,1 xTp:v:1,3 qx:v:0 dxo:a:0,0
+dTp:v:2,0,1 xTp:v:1,2 xTp:v:1,1 qf:v:0,1 dTe:a:2,0,0 xTp:v:1,0 dTe:a:2,0,1 add:v:1,1 dTp:v:2,1,0 xTe:a:1,2
+dTp:v:0,0,1 xTe:a:1,3 dxm:v:1,4,0 sdx:v:0,0,1 xTe:a:1,1 xTe:v:1,0 dTe:a:2,1,1 dxm:v:1,6,0 dxm:v:1,5,0
+dxm:v:1,7,0 qf:v:1,1 dxm:v:1,7,1 qf:v:2,1 dTe:a:2,1,0 sdx:v:0,1,1 dxm:v:1,6,1 dxm:v:1,4,1 dxm:v:1,7,2
+dxm:v:1,6,2 dxo:a:1,7 dxm:v:1,4,2 dxm:v:1,5,1 dxm:v:1,5,2 dxm:v:1,1,0 dxm:v:1,2,0 qt:v:2,0 dxo:v:1,6
+dxm:v:1,0,0 dxm:v:1,0,1 dxm:v:1,2,1 dxm:v:1,3,0 dxo:v:1,5 dwm:v:10,1,0 dxm:v:1,0,2 dxm:v:1,1,1 qx:v:1
+dxm:v:1,1,2 dxm:v:1,2,2 dxo:a:1,4 dxm:v:1,3,1 qt:v:2,1 dxo:v:1,0 dTe:a:0,0,0 dxm:v:1,3,2 sdx:v:0,1,0
+dTe:a:0,0,1 sdx:v:0,0,0 dxo:a:1,1 dwm:v:10,0,0 dwm:v:10,1,1 qt:v:1,0 dwm:v:5,1,0 sdx:v:1,1,1 dwm:v:9,0,0
+sdx:v:1,1,0 dwm:v:10,0,1 dxo:v:1,2 dTp:v:1,1,1 dxo:a:1,3 dTp:v:1,1,0 dwo:a:10,1 dwm:v:9,1,0 dwm:v:8,1,0
+qt:v:0,0 dTe:a:1,1,0 dwo:v:10,0 dwm:v:8,0,0 dTe:v:1,1,1 dwm:v:9,0,1 dwm:v:9,1,1 dwo:a:9,0 sdx:v:1,0,1
+dwm:v:8,1,1 dwo:a:9,1 sdw:v:10 qt:v:1,1 dwm:v:8,0,1 dTp:v:0,1,0 dwo:a:8,0 sdx:v:1,0,0 dTp:v:0,1,1 dwm:v:5,1,1
+dwm:v:5,0,0 dTe:a:0,1,0 dwm:v:5,0,1 dwm:v:6,1,0 dwm:v:6,1,1 dwo:v:8,1 sdw:v:9 dwm:v:6,0,0 dwo:a:5,0
+dwm:v:6,0,1 dwo:v:5,1 dwm:v:4,0,0 dwo:a:6,1 sdw:v:8 dwm:v:4,0,1 dwm:v:4,1,0 dTe:v:0,1,1 dwm:v:4,1,1
+dwm:v:11,1,0 dwm:v:11,0,0 dwo:v:6,0 dwo:a:4,0 qt:v:0,1 dwm:v:11,0,1 sdw:v:5 sdw:v:6 dwm:v:11,1,1 dwm:v:2,0,0
+dwo:v:4,1 dwo:a:11,0 dwm:v:2,0,1 dwm:v:2,1,0 sdw:v:4 dwm:v:2,1,1 dwm:v:0,1,0 dwo:v:11,1 dwm:v:0,0,0
+dwm:v:0,1,1 dwo:v:2,0 dwm:v:0,0,1 dwo:a:2,1 dwo:a:0,1 sdw:v:11 dwo:v:0,0 sdw:v:2 sdw:v:0 dwm:v:1,0,0
+dwm:v:1,1,0 dwm:v:1,0,1 dwm:v:1,1,1 dwo:v:1,0 dwo:v:1,1 sdw:v:1 dwm:v:3,1,0 dwm:v:3,1,1 dwm:v:3,0,0
+dwm:v:3,0,1 dwo:v:3,1 dwo:v:3,0 sdw:v:3 dwm:v:7,1,0 dwm:v:7,0,0 dwm:v:7,0,1 dwm:v:7,1,1 dwo:a:7,0 dwo:a:7,1
+sdw:v:7
 """
-LOADS = "w1 g w0 w2 x0 x1"
+LOADS = "w1 g w0 x0 w2 x1"
 
 
 def tile_pam_module_pa_v_kernel(
@@ -61,6 +62,8 @@ def tile_pam_module_pa_v_kernel(
         gnat = keep.tile([P, 6144], BF16, name="gnat", align_bytes=64)
         w_raw = [keep.tile([P, 4, C], BF16, name="w_raw%d" % g, align_bytes=64) for g in range(NG)]
         x_raw = [keep.tile([P, 16, 256], BF16, name="x_raw%d" % h, align_bytes=64) for h in range(2)]
+        ident_h = keep.tile([P, P], BF16, name="ident_h")
+        make_identity(nc, ident_h[:])
         ident = keep.tile([P, P], F32, name="ident")
         make_identity(nc, ident[:])
         nc.vector.memset(gnat[96:128, :], 0.0)
@@ -68,10 +71,9 @@ def tile_pam_module_pa_v_kernel(
         def load(name):
             i = int(name[1]) if len(name) > 1 else 0
             if name == "g":
-                nc.sync.dma_start(out=gnat[0:32, 0:3072], in_=grad_0.rearrange("n f v -> n (f v)"))
-                nc.scalar.dma_start(out=gnat[32:64, :], in_=grad_2[:, 0:512, :].rearrange("n f v -> n (f v)"))
-                nc.sync.dma_start(out=gnat[0:32, 3072:6144], in_=grad_1.rearrange("n f v -> n (f v)"))
-                nc.scalar.dma_start(out=gnat[64:96, :], in_=grad_2[:, 512:1024, :].rearrange("n f v -> n (f v)"))
+                nc.sync.dma_start(out=gnat[32:96, :], in_=grad_2.rearrange("n (k f) v -> (n k) (f v)", k=2))
+                nc.scalar.dma_start(out=gnat[0:32, 0:3072], in_=grad_0.rearrange("n f v -> n (f v)"))
+                nc.scalar.dma_start(out=gnat[0:32, 3072:6144], in_=grad_1.rearrange("n f v -> n (f v)"))
             elif name == "w0":
                 nc.sync.dma_start(out=w_raw[0][0:64], in_=Wq.rearrange("(p j) c -> p j c", j=4))
                 nc.sync.dma_start(out=w_raw[0][64:128], in_=Wk.rearrange("(p j) c -> p j c", j=4))
@@ -99,8 +101,8 @@ def tile_pam_module_pa_v_kernel(
         x_scales = keep.tile([P, 2, C], U8, name="x_scales", align_bytes=64)
         tiles = {}
 
-        def bank(key, shape):
-            b = psum.tile(shape, F32, name="bank", tag="bank", bufs=8)
+        def bank(key, shape, dtype=F32):
+            b = psum.tile(shape, dtype, name="bank", tag="bank", bufs=8)
             tiles[key] = b
             return b
 
@@ -115,24 +117,32 @@ def tile_pam_module_pa_v_kernel(
             else:
                 nc.vector.tensor_copy(out=out, in_=in_)
 
-        g_words = gnat[:].bitcast(F32).rearrange("q (m t w) -> q t w m", t=4, w=6)
+        g_cols = gnat[:].rearrange("q (m t v) -> q v t m", t=4, v=12)
 
         def gTp(en, w):
-            pg = bank(("g", w), [P, 4, P])
-            for t in range(4):
-                nc.tensor.transpose(pg[:, t, :], g_words[:, t, w, :], ident[:])
+            pg = bank(("g", w), [P, 8, P], BF16)
+            for a in range(2):
+                for t in range(4):
+                    nc.tensor.transpose(pg[:, 4 * a + t, :], g_cols[:, 2 * w + a, t, :], ident_h[:])
 
         def gTe(en, w):
-            src = tiles["g", w][:].rearrange("p t q -> p (t q)").bitcast(BF16)
-            src = src.rearrange("p (t q e) -> p q e t", t=4, e=2)[:, 0:96]
+            src = tiles["g", w][:].rearrange("p b q -> p q b")
             if w < 2:
-                out, factor = g_row[:, w], 0.125
+                out, factor = g_row[:, w].rearrange("p q a t -> p q (a t)"), 0.125
             else:
-                out, factor = g_col[:, :, 2 * (w - 2) : 2 * (w - 2) + 2, :], 0.25
-            if en == "a":
-                nc.scalar.activation(out=out, in_=src, func=COPY, scale=factor)
-            else:
-                nc.vector.tensor_scalar_mul(out, src, factor)
+                out, factor = g_col[:, :, 2 * (w - 2) : 2 * (w - 2) + 2, :].rearrange("p q a t -> p q (a t)"), 0.25
+            halves = (
+                (out[:, 0:32], src[:, 0:32]),
+                (
+                    out[:, 32:96].rearrange("p (k n) b -> p n k b", k=2),
+                    src[:, 32:96].rearrange("p (n k) b -> p n k b", k=2),
+                ),
+            )
+            for dst, part in halves:
+                if en == "a":
+                    nc.scalar.activation(out=dst, in_=part, func=COPY, scale=factor)
+                else:
+                    nc.vector.tensor_scalar_mul(dst, part, factor)
 
         def add(en, g, h):
             dz = stage(("dz", g, h), "dz", 4)
@@ -153,17 +163,17 @@ def tile_pam_module_pa_v_kernel(
             )
 
         def dTp(en, g, h, v):
-            words = tiles["dz", g, h][:].bitcast(F32).rearrange("p (u q e v) -> p u q e v", u=2, e=2, v=2)
-            pt = bank(("d", g, h, v), [P, 4, P])
-            for s in range(4):
-                nc.tensor.transpose(pt[:, s, :], words[:, s // 2, :, s % 2, v], ident[:])
+            cols = tiles["dz", g, h][:].rearrange("p (u q e t) -> p u q e t", u=2, e=2, t=4)
+            pt = bank(("d", g, h, v), [P, 8, P], BF16)
+            for b in range(8):
+                t, s = 2 * v + b // 4, b % 4
+                nc.tensor.transpose(pt[:, b, :], cols[:, s // 2, :, s % 2, t], ident_h[:])
 
         def dTe(en, g, h, v):
             if ("tok", g, h) not in tiles:
                 stage(("tok", g, h), "tok", 3)
-            dst = tiles["tok", g, h][:].rearrange("q (p v f s) -> q v p f s", v=2, f=2, s=4)
-            src = tiles["d", g, h, v][:].rearrange("q s p -> q (s p)").bitcast(BF16)
-            move(en, dst[:, v], src.rearrange("q (s p f) -> q p f s", s=4, f=2))
+            dst = tiles["tok", g, h][:].rearrange("q (p v b) -> q v p b", v=2, b=8)
+            move(en, dst[:, v], tiles["d", g, h, v][:].rearrange("q b p -> q p b"))
 
         def qt(en, g, h):
             cols = slice(512 * g, 512 * g + 512)
@@ -176,7 +186,7 @@ def tile_pam_module_pa_v_kernel(
             move(
                 en,
                 grouped[:].rearrange("p (e m j) -> p e m j", e=4, j=4),
-                w_raw[g][:].rearrange("p j (m e) -> p e m j", e=8)[:, 4 * k : 4 * k + 4],
+                w_raw[g][:, :, 512 * k : 512 * k + 512].rearrange("p j (m e) -> p e m j", e=4),
             )
 
         def qw(en, g, k):
@@ -224,16 +234,17 @@ def tile_pam_module_pa_v_kernel(
             )
 
         def dxo(en, h, e):
-            if ("dxt", h) not in tiles:
-                tiles["dxt", h] = work.tile([P, 16, 8, 32], F32, name="dx_out", tag="dx_out", bufs=2)
-            dst = tiles["dxt", h][:, :, e, :].rearrange("m n (u k) -> m n u k", u=2)
+            k = e // 4
+            if ("dxt", h, k) not in tiles:
+                tiles["dxt", h, k] = work.tile([P, 16, 4, 32], F32, name="dx_out", tag="dx_out", bufs=4)
+            dst = tiles["dxt", h, k][:, :, e % 4, :].rearrange("m n (u k) -> m n u k", u=2)
             move(en, dst, tiles["dx", h, e][:].rearrange("m (u n k) -> m n u k", u=2, n=16))
 
-        def sdx(en, h, k):
-            n0 = 16 * h + 4 * k
+        def sdx(en, h, k, i):
+            n0 = 16 * h + 8 * i
             nc.sync.dma_start(
-                out=out_0[n0 : n0 + 4].rearrange("n (m e) i j -> m n (e i j)", e=8),
-                in_=tiles["dxt", h][:, 4 * k : 4 * k + 4].rearrange("m n e t -> m n (e t)"),
+                out=out_0[n0 : n0 + 8, 512 * k : 512 * k + 512].rearrange("n (m e) i j -> m n (e i j)", e=4),
+                in_=tiles["dxt", h, k][:, 8 * i : 8 * i + 8].rearrange("m n e t -> m n (e t)"),
             )
 
         def dwm(en, oc, b, h):

@@ -19,34 +19,33 @@ FLOPS = 2 * 2 * T * C * J
 BYTES = 2 * (T * C + J * C + 32 * J * 12) + 4 * (T * C + J * C)
 
 PLAN = """
-wc:v:1,0 qw:v:1,0 wc:v:1,1 qw:v:1,1 gTp:v:4 gTe:v:4 gTp:v:2 gTp:v:1 gTe:a:2 gTp:v:3 wc:v:0,1 gTe:a:1 gTp:v:0
-wc:v:0,0 gTe:a:3 xs:v:0 gTe:a:0 gTp:v:5 gTe:a:5 qw:v:0,0 qw:v:0,1 add:v:0,0 xTp:v:0,2 add:v:1,0 qf:v:0,0
-xTe:a:0,2 xTp:v:0,3 xTp:v:0,0 wc:a:2,1 qf:v:1,0 xTe:v:0,3 dTp:v:0,0,0 xTp:v:0,1 dTp:v:1,0,0 dTp:v:1,0,1
-xTe:a:0,1 dTe:a:1,0,0 add:v:2,0 dxm:v:0,1,0 dxm:v:0,6,0 dxm:v:0,2,0 dxm:v:0,7,0 dxm:v:0,7,1 dTe:a:1,0,1
-qw:v:2,1 qf:v:2,0 dxm:v:0,5,0 xTe:v:0,0 wc:a:2,0 dxm:v:0,2,1 dxm:v:0,6,1 add:v:2,1 dxm:v:0,4,0 qw:v:2,0
-dxm:v:0,4,1 dxm:v:0,5,1 dxm:v:0,1,1 dxm:v:0,5,2 xs:v:1 dxm:v:0,6,2 dxo:a:0,5 add:v:0,1 dxm:v:0,4,2 dTp:v:2,0,0
-dxo:a:0,4 dxm:v:0,7,2 dxm:v:0,3,0 dxo:a:0,6 dxm:v:0,1,2 dxm:v:0,3,1 dxm:v:0,3,2 dxo:a:0,7 dxm:v:0,2,2
-dxm:v:0,0,0 dxm:v:0,0,1 dxo:a:0,3 dxo:v:0,2 dxm:v:0,0,2 dxo:a:0,1 dTp:v:2,1,1 xTp:v:1,3 qx:v:0 dxo:a:0,0
-dTp:v:2,0,1 xTp:v:1,2 xTp:v:1,1 qf:v:0,1 dTe:a:2,0,0 xTp:v:1,0 dTe:a:2,0,1 add:v:1,1 dTp:v:2,1,0 xTe:a:1,2
-dTp:v:0,0,1 xTe:a:1,3 dxm:v:1,4,0 sdx:v:0,0,1 xTe:a:1,1 xTe:v:1,0 dTe:a:2,1,1 dxm:v:1,6,0 dxm:v:1,5,0
-dxm:v:1,7,0 qf:v:1,1 dxm:v:1,7,1 qf:v:2,1 dTe:a:2,1,0 sdx:v:0,1,1 dxm:v:1,6,1 dxm:v:1,4,1 dxm:v:1,7,2
-dxm:v:1,6,2 dxo:a:1,7 dxm:v:1,4,2 dxm:v:1,5,1 dxm:v:1,5,2 dxm:v:1,1,0 dxm:v:1,2,0 qt:v:2,0 dxo:v:1,6
-dxm:v:1,0,0 dxm:v:1,0,1 dxm:v:1,2,1 dxm:v:1,3,0 dxo:v:1,5 dwm:v:10,1,0 dxm:v:1,0,2 dxm:v:1,1,1 qx:v:1
-dxm:v:1,1,2 dxm:v:1,2,2 dxo:a:1,4 dxm:v:1,3,1 qt:v:2,1 dxo:v:1,0 dTe:a:0,0,0 dxm:v:1,3,2 sdx:v:0,1,0
-dTe:a:0,0,1 sdx:v:0,0,0 dxo:a:1,1 dwm:v:10,0,0 dwm:v:10,1,1 qt:v:1,0 dwm:v:5,1,0 sdx:v:1,1,1 dwm:v:9,0,0
-sdx:v:1,1,0 dwm:v:10,0,1 dxo:v:1,2 dTp:v:1,1,1 dxo:a:1,3 dTp:v:1,1,0 dwo:a:10,1 dwm:v:9,1,0 dwm:v:8,1,0
-qt:v:0,0 dTe:a:1,1,0 dwo:v:10,0 dwm:v:8,0,0 dTe:v:1,1,1 dwm:v:9,0,1 dwm:v:9,1,1 dwo:a:9,0 sdx:v:1,0,1
-dwm:v:8,1,1 dwo:a:9,1 sdw:v:10 qt:v:1,1 dwm:v:8,0,1 dTp:v:0,1,0 dwo:a:8,0 sdx:v:1,0,0 dTp:v:0,1,1 dwm:v:5,1,1
-dwm:v:5,0,0 dTe:a:0,1,0 dwm:v:5,0,1 dwm:v:6,1,0 dwm:v:6,1,1 dwo:v:8,1 sdw:v:9 dwm:v:6,0,0 dwo:a:5,0
-dwm:v:6,0,1 dwo:v:5,1 dwm:v:4,0,0 dwo:a:6,1 sdw:v:8 dwm:v:4,0,1 dwm:v:4,1,0 dTe:v:0,1,1 dwm:v:4,1,1
-dwm:v:11,1,0 dwm:v:11,0,0 dwo:v:6,0 dwo:a:4,0 qt:v:0,1 dwm:v:11,0,1 sdw:v:5 sdw:v:6 dwm:v:11,1,1 dwm:v:2,0,0
-dwo:v:4,1 dwo:a:11,0 dwm:v:2,0,1 dwm:v:2,1,0 sdw:v:4 dwm:v:2,1,1 dwm:v:0,1,0 dwo:v:11,1 dwm:v:0,0,0
-dwm:v:0,1,1 dwo:v:2,0 dwm:v:0,0,1 dwo:a:2,1 dwo:a:0,1 sdw:v:11 dwo:v:0,0 sdw:v:2 sdw:v:0 dwm:v:1,0,0
-dwm:v:1,1,0 dwm:v:1,0,1 dwm:v:1,1,1 dwo:v:1,0 dwo:v:1,1 sdw:v:1 dwm:v:3,1,0 dwm:v:3,1,1 dwm:v:3,0,0
-dwm:v:3,0,1 dwo:v:3,1 dwo:v:3,0 sdw:v:3 dwm:v:7,1,0 dwm:v:7,0,0 dwm:v:7,0,1 dwm:v:7,1,1 dwo:a:7,0 dwo:a:7,1
-sdw:v:7
+wc:v:0,0 qw:v:0,0 wc:v:0,1 qw:v:0,1 gTp:v:5 gTe:v:5 gTp:v:4 gTp:v:1 wc:v:1,0 wc:a:1,1 gTp:v:3 gTe:v:4 gTp:v:0
+gTe:v:3 gTe:a:1 xs:v:0 gTe:a:0 gTp:v:2 gTe:a:2 qw:v:1,0 qw:v:1,1 xTp:v:0,3 xTp:v:0,1 add:v:1,0 add:v:0,0
+xTp:v:0,2 add:v:2,0 xTe:a:0,3 dTp:v:1,0,1 wc:a:2,1 xTp:v:0,0 qf:v:1,0 dTp:v:1,0,0 dTp:v:0,0,1 dTp:v:2,0,1
+xTe:a:0,1 xTe:a:0,2 dTe:a:1,0,0 qf:v:0,0 dTe:v:1,0,1 dTp:v:2,0,0 qw:v:2,1 dxm:v:0,7,0 dTp:v:0,0,0 dxm:v:0,5,0
+wc:a:2,0 qf:v:2,0 dxm:v:0,6,0 dxm:v:0,5,1 dxm:v:0,6,1 dxm:v:0,7,1 xTe:a:0,0 dxm:v:0,7,2 dxm:v:0,6,2 qw:v:2,0
+dxm:v:0,5,2 dTe:a:0,0,0 dxm:v:0,0,0 add:v:0,1 dxo:a:0,6 dxm:v:0,0,1 dxm:v:0,4,0 dxm:v:0,0,2 add:v:1,1
+dxm:v:0,1,0 dTe:a:2,0,0 dxm:v:0,4,1 dxm:v:0,1,1 dxm:v:0,4,2 dxo:a:0,5 dxm:v:0,1,2 dxm:v:0,2,0 qf:v:0,1
+dxm:v:0,2,1 dxm:v:0,3,0 dxo:a:0,7 dxm:v:0,2,2 dxo:a:0,4 sdx:v:0,1,1 qf:v:1,1 dxm:v:0,3,1 dxo:a:0,1 dTp:v:0,1,1
+add:v:2,1 dxm:v:1,5,0 dTe:a:0,0,1 dxo:a:0,2 dxm:v:0,3,2 dxm:v:1,6,0 dxm:v:1,6,1 dxm:v:1,7,0 dxm:v:1,5,1
+dxo:a:0,3 dxm:v:1,7,1 dxo:a:0,0 qt:v:1,0 dxm:v:1,4,0 dxm:v:1,4,1 dTe:a:2,0,1 dxm:v:1,1,0 dxm:v:1,1,1 qf:v:2,1
+xs:v:1 dxm:v:1,0,0 dxm:v:1,0,1 dxm:v:1,7,2 dxo:v:1,7 dTe:a:0,1,1 dxm:v:1,6,2 dxm:v:1,0,2 dxm:v:1,4,2
+dxm:v:1,1,2 dxm:v:1,5,2 dxo:v:1,4 sdx:v:0,1,0 dxo:a:1,6 dxm:v:1,2,0 dxo:a:1,5 dxm:v:1,3,0 xTp:v:1,1
+dTp:v:2,1,0 qt:v:0,0 dTp:v:0,1,0 qx:v:0 xTp:v:1,2 dxm:v:1,2,1 dxo:a:1,1 dxm:v:1,2,2 qt:v:2,0 dxm:v:1,3,1
+dTe:v:0,1,0 dxm:v:1,3,2 xTp:v:1,3 xTp:v:1,0 dxo:a:1,0 dTe:a:2,1,0 sdx:v:0,0,1 xTe:a:1,2 dxo:v:1,2 dTp:v:2,1,1
+sdx:v:0,0,0 xTe:a:1,1 sdx:v:1,1,1 qt:v:0,1 dTp:v:1,1,1 sdx:v:1,1,0 dxo:a:1,3 dwm:v:2,1,0 dwm:v:8,0,0
+dwm:v:9,1,0 xTe:a:1,3 dwm:v:8,1,0 xTe:v:1,0 dTe:a:2,1,1 dwm:v:2,0,0 qx:v:1 dwm:v:2,1,1 qt:v:2,1 dwm:v:2,0,1
+dwm:v:8,1,1 dwo:v:2,1 sdx:v:1,0,0 dwm:v:10,1,0 dwm:v:9,1,1 sdx:v:1,0,1 dwm:v:8,0,1 dwm:v:9,0,0 dwm:v:9,0,1
+dwo:a:2,0 dwm:v:10,1,1 dTp:v:1,1,0 dwm:v:10,0,0 dwo:v:8,1 dwo:a:8,0 dwm:v:10,0,1 dTe:v:1,1,1 dwm:v:3,0,0
+dwo:v:9,1 dwo:a:9,0 dwm:v:3,1,0 dwo:a:10,1 dwm:v:11,1,0 dwm:v:3,0,1 dwo:a:10,0 sdw:v:2 dwm:v:3,1,1 dTe:v:1,1,0
+sdw:v:8 dwo:a:3,0 dwm:v:11,1,1 dwm:v:4,0,0 sdw:v:9 dwo:v:3,1 qt:v:1,1 sdw:v:10 dwo:v:11,1 dwm:v:11,0,0 sdw:v:3
+dwm:v:5,0,0 dwm:v:11,0,1 dwm:v:5,1,0 dwm:v:5,0,1 dwo:a:11,0 dwm:v:5,1,1 sdw:v:11 dwo:a:5,0 dwm:v:6,0,0
+dwm:v:4,0,1 dwo:a:5,1 dwm:v:4,1,0 dwo:v:4,0 dwm:v:1,0,0 dwm:v:4,1,1 sdw:v:5 dwo:a:4,1 sdw:v:4 dwm:v:6,0,1
+dwm:v:7,1,0 dwm:v:6,1,0 dwo:a:6,0 dwm:v:7,0,0 dwm:v:6,1,1 dwo:v:6,1 dwm:v:7,0,1 dwm:v:1,1,0 dwo:a:7,0
+dwm:v:1,0,1 dwm:v:7,1,1 sdw:v:6 dwo:v:7,1 dwm:v:1,1,1 dwo:a:1,1 sdw:v:7 dwo:a:1,0 sdw:v:1 dwm:v:0,0,0
+dwm:v:0,1,0 dwm:v:0,1,1 dwm:v:0,0,1 dwo:a:0,0 dwo:v:0,1 sdw:v:0
 """
-LOADS = "w1 g w0 x0 w2 x1"
+LOADS = "w0 g w1 x0 w2 x1"
 
 
 def tile_pam_module_pa_v_kernel(
@@ -62,8 +61,6 @@ def tile_pam_module_pa_v_kernel(
         gnat = keep.tile([P, 6144], BF16, name="gnat", align_bytes=64)
         w_raw = [keep.tile([P, 4, C], BF16, name="w_raw%d" % g, align_bytes=64) for g in range(NG)]
         x_raw = [keep.tile([P, 16, 256], BF16, name="x_raw%d" % h, align_bytes=64) for h in range(2)]
-        ident_h = keep.tile([P, P], BF16, name="ident_h")
-        make_identity(nc, ident_h[:])
         ident = keep.tile([P, P], F32, name="ident")
         make_identity(nc, ident[:])
         nc.vector.memset(gnat[96:128, :], 0.0)
@@ -117,25 +114,25 @@ def tile_pam_module_pa_v_kernel(
             else:
                 nc.vector.tensor_copy(out=out, in_=in_)
 
-        g_cols = gnat[:].rearrange("q (m t v) -> q v t m", t=4, v=12)
+        g_words = gnat[:].bitcast(F32).rearrange("q (m t w) -> q t w m", t=4, w=6)
 
         def gTp(en, w):
-            pg = bank(("g", w), [P, 8, P], BF16)
-            for a in range(2):
-                for t in range(4):
-                    nc.tensor.transpose(pg[:, 4 * a + t, :], g_cols[:, 2 * w + a, t, :], ident_h[:])
+            pg = bank(("g", w), [P, 4, P])
+            for t in range(4):
+                nc.tensor.transpose(pg[:, t, :], g_words[:, t, w, :], ident[:])
 
         def gTe(en, w):
-            src = tiles["g", w][:].rearrange("p b q -> p q b")
+            src = tiles["g", w][:].rearrange("p t q -> p (t q)").bitcast(BF16)
+            src = src.rearrange("p (t q a) -> p q a t", t=4, a=2)
             if w < 2:
-                out, factor = g_row[:, w].rearrange("p q a t -> p q (a t)"), 0.125
+                out, factor = g_row[:, w], 0.125
             else:
-                out, factor = g_col[:, :, 2 * (w - 2) : 2 * (w - 2) + 2, :].rearrange("p q a t -> p q (a t)"), 0.25
+                out, factor = g_col[:, :, 2 * (w - 2) : 2 * (w - 2) + 2, :], 0.25
             halves = (
                 (out[:, 0:32], src[:, 0:32]),
                 (
-                    out[:, 32:96].rearrange("p (k n) b -> p n k b", k=2),
-                    src[:, 32:96].rearrange("p (n k) b -> p n k b", k=2),
+                    out[:, 32:96].rearrange("p (k n) a t -> p n k a t", k=2),
+                    src[:, 32:96].rearrange("p (n k) a t -> p n k a t", k=2),
                 ),
             )
             for dst, part in halves:
@@ -147,12 +144,14 @@ def tile_pam_module_pa_v_kernel(
         def add(en, g, h):
             dz = stage(("dz", g, h), "dz", 4)
             q0 = 32 * g + 16 * h
-            shape = [P, 16, 2, 8, 4]
+            row_shape, col_shape = [P, 32, 8, 4], [P, 16, 2, 32]
+            col = g_col[:, q0 : q0 + 16].rearrange("p n j t -> p n (j t)").unsqueeze(2).to_broadcast(col_shape)
             for u in range(2):
+                row = g_row[:, u, q0 : q0 + 16].rearrange("p n a t -> p (n a) t")
                 nc.vector.tensor_tensor(
-                    out=dz[:, 1024 * u : 1024 * (u + 1)].rearrange("p (n a j t) -> p n a j t", n=16, a=2, j=8),
-                    in0=g_row[:, u, q0 : q0 + 16].unsqueeze(3).to_broadcast(shape),
-                    in1=g_col[:, q0 : q0 + 16].unsqueeze(2).to_broadcast(shape),
+                    out=dz[:, 1024 * u : 1024 * (u + 1)].rearrange("p (e q t) -> p q e t", e=2, t=4),
+                    in0=row.unsqueeze(2).to_broadcast(row_shape),
+                    in1=col,
                     op=ADD,
                 )
 
@@ -163,17 +162,17 @@ def tile_pam_module_pa_v_kernel(
             )
 
         def dTp(en, g, h, v):
-            cols = tiles["dz", g, h][:].rearrange("p (u q e t) -> p u q e t", u=2, e=2, t=4)
-            pt = bank(("d", g, h, v), [P, 8, P], BF16)
-            for b in range(8):
-                t, s = 2 * v + b // 4, b % 4
-                nc.tensor.transpose(pt[:, b, :], cols[:, s // 2, :, s % 2, t], ident_h[:])
+            words = tiles["dz", g, h][:].bitcast(F32).rearrange("p (s q v) -> p s q v", s=4, v=2)
+            pt = bank(("d", g, h, v), [P, 4, P])
+            for s in range(4):
+                nc.tensor.transpose(pt[:, s, :], words[:, s, :, v], ident[:])
 
         def dTe(en, g, h, v):
             if ("tok", g, h) not in tiles:
                 stage(("tok", g, h), "tok", 3)
-            dst = tiles["tok", g, h][:].rearrange("q (p v b) -> q v p b", v=2, b=8)
-            move(en, dst[:, v], tiles["d", g, h, v][:].rearrange("q b p -> q p b"))
+            dst = tiles["tok", g, h][:].rearrange("q (p v f s) -> q v p f s", v=2, f=2, s=4)
+            src = tiles["d", g, h, v][:].rearrange("q s p -> q (s p)").bitcast(BF16)
+            move(en, dst[:, v], src.rearrange("q (s p f) -> q p f s", s=4, f=2))
 
         def qt(en, g, h):
             cols = slice(512 * g, 512 * g + 512)
@@ -237,8 +236,8 @@ def tile_pam_module_pa_v_kernel(
             k = e // 4
             if ("dxt", h, k) not in tiles:
                 tiles["dxt", h, k] = work.tile([P, 16, 4, 32], F32, name="dx_out", tag="dx_out", bufs=4)
-            dst = tiles["dxt", h, k][:, :, e % 4, :].rearrange("m n (u k) -> m n u k", u=2)
-            move(en, dst, tiles["dx", h, e][:].rearrange("m (u n k) -> m n u k", u=2, n=16))
+            dst = tiles["dxt", h, k][:, :, e % 4, :].rearrange("m n (u k e) -> m u n k e", u=2, e=2)
+            move(en, dst, tiles["dx", h, e][:].rearrange("m (u e n k) -> m u n k e", u=2, e=2, n=16))
 
         def sdx(en, h, k, i):
             n0 = 16 * h + 8 * i

@@ -19,33 +19,32 @@ FLOPS = 2 * 2 * T * C * J
 BYTES = 2 * (T * C + J * C + 32 * J * 12) + 4 * (T * C + J * C)
 
 PLAN = """
-wc:v:0,0 qw:v:0,0 wc:v:0,1 qw:v:0,1 gTp:v:5 gTe:v:5 gTp:v:4 gTp:v:1 wc:v:1,0 wc:a:1,1 gTp:v:3 gTe:v:4 gTp:v:0
-gTe:v:3 gTe:a:1 xs:v:0 gTe:a:0 gTp:v:2 gTe:a:2 qw:v:1,0 qw:v:1,1 xTp:v:0,3 xTp:v:0,1 add:v:1,0 add:v:0,0
-xTp:v:0,2 add:v:2,0 xTe:a:0,3 dTp:v:1,0,1 wc:a:2,1 xTp:v:0,0 qf:v:1,0 dTp:v:1,0,0 dTp:v:0,0,1 dTp:v:2,0,1
-xTe:a:0,1 xTe:a:0,2 dTe:a:1,0,0 qf:v:0,0 dTe:v:1,0,1 dTp:v:2,0,0 qw:v:2,1 dxm:v:0,7,0 dTp:v:0,0,0 dxm:v:0,5,0
-wc:a:2,0 qf:v:2,0 dxm:v:0,6,0 dxm:v:0,5,1 dxm:v:0,6,1 dxm:v:0,7,1 xTe:a:0,0 dxm:v:0,7,2 dxm:v:0,6,2 qw:v:2,0
-dxm:v:0,5,2 dTe:a:0,0,0 dxm:v:0,0,0 add:v:0,1 dxo:a:0,6 dxm:v:0,0,1 dxm:v:0,4,0 dxm:v:0,0,2 add:v:1,1
-dxm:v:0,1,0 dTe:a:2,0,0 dxm:v:0,4,1 dxm:v:0,1,1 dxm:v:0,4,2 dxo:a:0,5 dxm:v:0,1,2 dxm:v:0,2,0 qf:v:0,1
-dxm:v:0,2,1 dxm:v:0,3,0 dxo:a:0,7 dxm:v:0,2,2 dxo:a:0,4 sdx:v:0,1,1 qf:v:1,1 dxm:v:0,3,1 dxo:a:0,1 dTp:v:0,1,1
-add:v:2,1 dxm:v:1,5,0 dTe:a:0,0,1 dxo:a:0,2 dxm:v:0,3,2 dxm:v:1,6,0 dxm:v:1,6,1 dxm:v:1,7,0 dxm:v:1,5,1
-dxo:a:0,3 dxm:v:1,7,1 dxo:a:0,0 qt:v:1,0 dxm:v:1,4,0 dxm:v:1,4,1 dTe:a:2,0,1 dxm:v:1,1,0 dxm:v:1,1,1 qf:v:2,1
-xs:v:1 dxm:v:1,0,0 dxm:v:1,0,1 dxm:v:1,7,2 dxo:v:1,7 dTe:a:0,1,1 dxm:v:1,6,2 dxm:v:1,0,2 dxm:v:1,4,2
-dxm:v:1,1,2 dxm:v:1,5,2 dxo:v:1,4 sdx:v:0,1,0 dxo:a:1,6 dxm:v:1,2,0 dxo:a:1,5 dxm:v:1,3,0 xTp:v:1,1
-dTp:v:2,1,0 qt:v:0,0 dTp:v:0,1,0 qx:v:0 xTp:v:1,2 dxm:v:1,2,1 dxo:a:1,1 dxm:v:1,2,2 qt:v:2,0 dxm:v:1,3,1
-dTe:v:0,1,0 dxm:v:1,3,2 xTp:v:1,3 xTp:v:1,0 dxo:a:1,0 dTe:a:2,1,0 sdx:v:0,0,1 xTe:a:1,2 dxo:v:1,2 dTp:v:2,1,1
-sdx:v:0,0,0 xTe:a:1,1 sdx:v:1,1,1 qt:v:0,1 dTp:v:1,1,1 sdx:v:1,1,0 dxo:a:1,3 dwm:v:2,1,0 dwm:v:8,0,0
-dwm:v:9,1,0 xTe:a:1,3 dwm:v:8,1,0 xTe:v:1,0 dTe:a:2,1,1 dwm:v:2,0,0 qx:v:1 dwm:v:2,1,1 qt:v:2,1 dwm:v:2,0,1
-dwm:v:8,1,1 dwo:v:2,1 sdx:v:1,0,0 dwm:v:10,1,0 dwm:v:9,1,1 sdx:v:1,0,1 dwm:v:8,0,1 dwm:v:9,0,0 dwm:v:9,0,1
-dwo:a:2,0 dwm:v:10,1,1 dTp:v:1,1,0 dwm:v:10,0,0 dwo:v:8,1 dwo:a:8,0 dwm:v:10,0,1 dTe:v:1,1,1 dwm:v:3,0,0
-dwo:v:9,1 dwo:a:9,0 dwm:v:3,1,0 dwo:a:10,1 dwm:v:11,1,0 dwm:v:3,0,1 dwo:a:10,0 sdw:v:2 dwm:v:3,1,1 dTe:v:1,1,0
-sdw:v:8 dwo:a:3,0 dwm:v:11,1,1 dwm:v:4,0,0 sdw:v:9 dwo:v:3,1 qt:v:1,1 sdw:v:10 dwo:v:11,1 dwm:v:11,0,0 sdw:v:3
-dwm:v:5,0,0 dwm:v:11,0,1 dwm:v:5,1,0 dwm:v:5,0,1 dwo:a:11,0 dwm:v:5,1,1 sdw:v:11 dwo:a:5,0 dwm:v:6,0,0
-dwm:v:4,0,1 dwo:a:5,1 dwm:v:4,1,0 dwo:v:4,0 dwm:v:1,0,0 dwm:v:4,1,1 sdw:v:5 dwo:a:4,1 sdw:v:4 dwm:v:6,0,1
-dwm:v:7,1,0 dwm:v:6,1,0 dwo:a:6,0 dwm:v:7,0,0 dwm:v:6,1,1 dwo:v:6,1 dwm:v:7,0,1 dwm:v:1,1,0 dwo:a:7,0
-dwm:v:1,0,1 dwm:v:7,1,1 sdw:v:6 dwo:v:7,1 dwm:v:1,1,1 dwo:a:1,1 sdw:v:7 dwo:a:1,0 sdw:v:1 dwm:v:0,0,0
-dwm:v:0,1,0 dwm:v:0,1,1 dwm:v:0,0,1 dwo:a:0,0 dwo:v:0,1 sdw:v:0
+wc:a:1,1 lwk:a: qw:v:1,1 gTp:v:4 wc:v:1,0 gTp:v:5 qw:v:1,0 gTe:a:4 gTe:a:5 gTp:v:0 gTp:v:1 gTp:v:3 gTe:a:0 gTp:v:2
+gTe:a:1 gTe:a:3 gTe:a:2 wc:v:2,1 wc:v:2,0 xs:a:0 xTp:v:0,0 wc:a:0,0 qw:v:2,1 add:v:0,0 add:v:1,0 xTp:v:0,2
+add:v:2,0 qf:v:1,0 dTp:v:0,0,0 xTe:a:0,0 qf:v:0,0 qw:v:0,0 wc:a:0,1 xTe:v:0,2 dTp:v:1,0,1 dTp:v:1,0,0
+xTp:v:0,3 dTp:v:0,0,1 xTe:v:0,3 dxm:v:0,3,0 dxm:v:0,2,0 dxm:v:0,2,1 dxm:v:0,1,0 dxm:v:0,1,1 dxm:v:0,3,1
+qf:v:2,0 dxm:v:0,0,0 dxm:v:0,0,1 qw:v:2,0 qw:v:0,1 dxm:v:0,1,2 dxm:v:0,3,2 dxm:v:0,2,2 dTe:a:0,0,0 add:v:1,1
+dxm:v:0,0,2 dxm:v:0,6,0 dxm:v:0,6,1 dxo:a:0,1 dxm:v:0,6,2 dxm:v:0,4,0 dxo:a:0,3 dxo:a:0,0 dxm:v:0,4,1
+dxm:v:0,4,2 dxm:v:0,5,0 add:v:0,1 dxo:a:0,2 dxo:a:0,4 dxm:v:0,5,1 qf:v:1,1 dxo:a:0,6 sdx:v:0,0,0 dxm:v:0,7,0
+dxm:v:0,5,2 dxm:v:0,7,1 dxm:v:0,7,2 xTp:v:0,1 dxo:a:0,5 qf:v:0,1 add:v:2,1 dTp:v:0,1,1 dxo:a:0,7 dTe:a:0,0,1
+qf:v:2,1 dTp:v:2,0,0 xTe:a:0,1 dTp:v:0,1,0 dxm:v:1,3,0 dxm:v:1,0,0 dTe:a:1,0,1 dxm:v:1,0,1 dTe:v:0,1,1
+dxm:v:1,3,1 dxm:v:1,1,0 dTe:a:0,1,0 dxm:v:1,1,1 dxm:v:1,2,0 dxm:v:1,2,1 dxm:v:1,3,2 dxm:v:1,0,2 qt:v:0,0
+dxo:a:1,3 dxm:v:1,1,2 dxm:v:1,2,2 dxm:v:1,5,0 dxm:v:1,6,0 dxm:v:1,6,1 dxo:a:1,0 dxm:v:1,6,2 sdx:v:0,0,1
+dxm:v:1,7,0 dxo:a:1,2 dxo:v:1,1 dxm:v:1,5,1 dxm:v:1,4,0 xs:v:1 dxm:v:1,4,1 dxm:v:1,4,2 dTe:a:1,0,0 qx:v:0
+dxm:v:1,5,2 dxm:v:1,7,1 sdx:v:0,1,1 dxm:v:1,7,2 xTp:v:1,3 qt:v:0,1 sdx:v:0,1,0 xTp:v:1,1 xTp:v:1,2 dxo:a:1,6
+xTp:v:1,0 dxo:a:1,4 dxo:a:1,7 xTe:a:1,3 sdx:v:1,0,0 dxo:v:1,5 xTe:v:1,1 xTe:v:1,2 sdx:v:1,0,1 xTe:a:1,0
+dTp:v:1,1,1 dTp:v:2,0,1 dTp:v:1,1,0 dwm:v:3,1,0 sdx:v:1,1,1 dwm:v:3,0,0 qx:v:1 dTe:a:2,0,0 qt:v:1,0
+dwm:v:3,0,1 dwm:v:3,1,1 dwo:v:3,0 dTe:v:1,1,1 dTe:v:1,1,0 dwo:a:3,1 dwm:v:2,1,0 dwm:v:0,0,0 dwm:v:0,0,1
+dwo:a:0,0 dwm:v:0,1,0 dwm:v:0,1,1 dwm:v:1,0,0 dwm:v:1,0,1 dwm:v:1,1,0 dwm:v:2,0,0 qt:v:1,1 dwm:v:1,1,1
+dwo:a:0,1 dwo:a:1,0 dwm:v:6,0,0 dwo:a:1,1 dwm:v:2,0,1 dwm:v:2,1,1 dwm:v:5,0,0 dwm:v:5,1,0 sdx:v:1,1,0
+dwm:v:5,1,1 sdw:v:3 dwm:v:6,1,0 dwo:a:2,1 dwm:v:6,0,1 sdw:v:0 dwm:v:5,0,1 dwo:v:2,0 dwm:v:6,1,1 dTp:v:2,1,1
+dTp:v:2,1,0 dwo:v:5,1 dwm:v:4,1,0 dTe:a:2,0,1 dwo:a:5,0 dwo:v:6,0 sdw:v:1 dwo:a:6,1 dwm:v:4,0,0 dwm:v:4,1,1
+sdw:v:2 dwm:v:4,0,1 sdw:v:5 dTe:a:2,1,1 dwm:v:7,1,0 qt:v:2,0 dwm:v:7,1,1 dTe:v:2,1,0 dwm:v:7,0,0 sdw:v:6
+dwo:v:4,1 dwm:v:7,0,1 dwo:a:4,0 dwm:v:9,0,0 qt:v:2,1 sdw:v:4 dwm:v:9,0,1 dwo:a:7,1 dwm:v:9,1,0 dwo:a:7,0
+sdw:v:7 dwo:a:9,0 dwm:v:9,1,1 dwo:v:9,1 sdw:v:9 dwm:v:11,0,0 dwm:v:11,1,0 dwm:v:11,1,1 dwo:a:11,1 dwm:v:11,0,1
+dwo:v:11,0 sdw:v:11 dwm:v:10,1,0 dwm:v:10,1,1 dwo:v:10,1 dwm:v:10,0,0 dwm:v:10,0,1 dwo:v:10,0 sdw:v:10
+dwm:v:8,1,0 dwm:v:8,0,0 dwm:v:8,0,1 dwm:v:8,1,1 dwo:a:8,0 dwo:a:8,1 sdw:v:8
 """
-LOADS = "w0 g w1 x0 w2 x1"
 
 
 def tile_pam_module_pa_v_kernel(
@@ -65,26 +64,21 @@ def tile_pam_module_pa_v_kernel(
         make_identity(nc, ident[:])
         nc.vector.memset(gnat[96:128, :], 0.0)
 
-        def load(name):
-            i = int(name[1]) if len(name) > 1 else 0
-            if name == "g":
-                nc.sync.dma_start(out=gnat[32:96, :], in_=grad_2.rearrange("n (k f) v -> (n k) (f v)", k=2))
-                nc.scalar.dma_start(out=gnat[0:32, 0:3072], in_=grad_0.rearrange("n f v -> n (f v)"))
-                nc.scalar.dma_start(out=gnat[0:32, 3072:6144], in_=grad_1.rearrange("n f v -> n (f v)"))
-            elif name == "w0":
-                nc.sync.dma_start(out=w_raw[0][0:64], in_=Wq.rearrange("(p j) c -> p j c", j=4))
-                nc.sync.dma_start(out=w_raw[0][64:128], in_=Wk.rearrange("(p j) c -> p j c", j=4))
-            elif name[0] == "w":
-                nc.sync.dma_start(
-                    out=w_raw[i][:], in_=Wv[512 * i - 512 : 512 * i, :].rearrange("(p j) c -> p j c", j=4)
-                )
-            else:
-                nc.sync.dma_start(
-                    out=x_raw[i][:], in_=x[16 * i : 16 * i + 16].rearrange("n (p e) i j -> p n (e i j)", e=8)
-                )
+        rows = "(p j) c -> p j c"
+        grad = "n f v -> n (f v)"
+        half = slice(0, 512), slice(512, 1024)
+        nc.scalar.dma_start(out=gnat[0:32, 0:3072], in_=grad_0.rearrange(grad))
+        nc.scalar.dma_start(out=gnat[0:32, 3072:6144], in_=grad_1.rearrange(grad))
+        nc.sync.dma_start(out=w_raw[1][:, :, half[1]], in_=Wv[0:512, half[1]].rearrange(rows, j=4))
+        nc.sync.dma_start(out=gnat[32:96, :], in_=grad_2.rearrange("n (k f) v -> (n k) (f v)", k=2))
+        nc.sync.dma_start(out=w_raw[1][:, :, half[0]], in_=Wv[0:512, half[0]].rearrange(rows, j=4))
+        nc.sync.dma_start(out=w_raw[2][:], in_=Wv[512:1024, :].rearrange(rows, j=4))
+        nc.sync.dma_start(out=x_raw[0][:], in_=x[0:16].rearrange("n (p e) i j -> p n (e i j)", e=8))
+        nc.sync.dma_start(out=w_raw[0][0:64], in_=Wq.rearrange(rows, j=4))
+        nc.sync.dma_start(out=x_raw[1][:], in_=x[16:32].rearrange("n (p e) i j -> p n (e i j)", e=8))
 
-        for name in LOADS.split():
-            load(name)
+        def lwk(en):
+            nc.scalar.dma_start(out=w_raw[0][64:128], in_=Wk.rearrange(rows, j=4))
 
         g_row = keep.tile([P, 2, 96, 2, 4], BF16, name="g_row", align_bytes=64)
         g_col = keep.tile([P, 96, 8, 4], BF16, name="g_col", align_bytes=64)
@@ -196,9 +190,10 @@ def tile_pam_module_pa_v_kernel(
 
         def xs(en, h):
             xr = stage(("xr", h), "xr", 1)
-            nc.vector.tensor_copy(
-                out=xr[:].rearrange("p (b n k) -> p b n k", b=16, n=16),
-                in_=x_raw[h][:].rearrange("p n (b k) -> p b n k", k=16),
+            move(
+                en,
+                xr[:].rearrange("p (b n k) -> p b n k", b=16, n=16),
+                x_raw[h][:].rearrange("p n (b k) -> p b n k", k=16),
             )
 
         def xTp(en, h, k):
@@ -277,9 +272,9 @@ def tile_pam_module_pa_v_kernel(
 
         steps = {
             "gTp": gTp, "gTe": gTe, "add": add, "qf": qf, "dTp": dTp, "dTe": dTe, "qt": qt, "wc": wc, "qw": qw,
-            "xs": xs, "xTp": xTp, "xTe": xTe, "qx": qx, "dxm": dxm, "dxo": dxo, "sdx": sdx, "dwm": dwm, "dwo": dwo,
+            "lwk": lwk, "xs": xs, "xTp": xTp, "xTe": xTe, "qx": qx, "dxm": dxm, "dxo": dxo, "sdx": sdx, "dwm": dwm, "dwo": dwo,
             "sdw": sdw,
         }
         for step in PLAN.split():
             name, engine, where = step.split(":")
-            steps[name](engine, *[int(i) for i in where.split(",")])
+            steps[name](engine, *[int(i) for i in where.split(",") if i])

@@ -13,37 +13,38 @@ COPY = mybir.ActivationFunctionType.Copy
 ADD = mybir.AluOpType.add
 
 P = 128
-T, C, J = 1024, 1024, 1536
-NG = 3
-FLOPS = 2 * 2 * T * C * J
-BYTES = 2 * (T * C + J * C + 32 * J * 12) + 4 * (T * C + J * C)
+BATCH, ROWS, COLS = 32, 4, 8
+TOKENS, CHANNELS, FEATURES = BATCH * ROWS * COLS, 1024, 1536
+PASS = 512
+FEATURE_PASSES = FEATURES // PASS
+TOKEN_PASSES = TOKENS // PASS
+PASS_IMAGES = BATCH // TOKEN_PASSES
+POOLED = ROWS + COLS
+GRAD_ROWS = FEATURE_PASSES * BATCH
+BANK = 512
 
-PLAN = """
-wc:a:1,1 lwk:a: qw:v:1,1 gTp:v:4 wc:v:1,0 gTp:v:5 qw:v:1,0 gTe:a:4 gTe:a:5 gTp:v:0 gTp:v:1 gTp:v:3 gTe:a:0 gTp:v:2
-gTe:a:1 gTe:a:3 gTe:a:2 wc:v:2,1 wc:v:2,0 xs:a:0 xTp:v:0,0 wc:a:0,0 qw:v:2,1 add:v:0,0 add:v:1,0 xTp:v:0,2
-add:v:2,0 qf:v:1,0 dTp:v:0,0,0 xTe:a:0,0 qf:v:0,0 qw:v:0,0 wc:a:0,1 xTe:v:0,2 dTp:v:1,0,1 dTp:v:1,0,0
-xTp:v:0,3 dTp:v:0,0,1 xTe:v:0,3 dxm:v:0,3,0 dxm:v:0,2,0 dxm:v:0,2,1 dxm:v:0,1,0 dxm:v:0,1,1 dxm:v:0,3,1
-qf:v:2,0 dxm:v:0,0,0 dxm:v:0,0,1 qw:v:2,0 qw:v:0,1 dxm:v:0,1,2 dxm:v:0,3,2 dxm:v:0,2,2 dTe:a:0,0,0 add:v:1,1
-dxm:v:0,0,2 dxm:v:0,6,0 dxm:v:0,6,1 dxo:a:0,1 dxm:v:0,6,2 dxm:v:0,4,0 dxo:a:0,3 dxo:a:0,0 dxm:v:0,4,1
-dxm:v:0,4,2 dxm:v:0,5,0 add:v:0,1 dxo:a:0,2 dxo:a:0,4 dxm:v:0,5,1 qf:v:1,1 dxo:a:0,6 sdx:v:0,0,0 dxm:v:0,7,0
-dxm:v:0,5,2 dxm:v:0,7,1 dxm:v:0,7,2 xTp:v:0,1 dxo:a:0,5 qf:v:0,1 add:v:2,1 dTp:v:0,1,1 dxo:a:0,7 dTe:a:0,0,1
-qf:v:2,1 dTp:v:2,0,0 xTe:a:0,1 dTp:v:0,1,0 dxm:v:1,3,0 dxm:v:1,0,0 dTe:a:1,0,1 dxm:v:1,0,1 dTe:v:0,1,1
-dxm:v:1,3,1 dxm:v:1,1,0 dTe:a:0,1,0 dxm:v:1,1,1 dxm:v:1,2,0 dxm:v:1,2,1 dxm:v:1,3,2 dxm:v:1,0,2 qt:v:0,0
-dxo:a:1,3 dxm:v:1,1,2 dxm:v:1,2,2 dxm:v:1,5,0 dxm:v:1,6,0 dxm:v:1,6,1 dxo:a:1,0 dxm:v:1,6,2 sdx:v:0,0,1
-dxm:v:1,7,0 dxo:a:1,2 dxo:v:1,1 dxm:v:1,5,1 dxm:v:1,4,0 xs:v:1 dxm:v:1,4,1 dxm:v:1,4,2 dTe:a:1,0,0 qx:v:0
-dxm:v:1,5,2 dxm:v:1,7,1 sdx:v:0,1,1 dxm:v:1,7,2 xTp:v:1,3 qt:v:0,1 sdx:v:0,1,0 xTp:v:1,1 xTp:v:1,2 dxo:a:1,6
-xTp:v:1,0 dxo:a:1,4 dxo:a:1,7 xTe:a:1,3 sdx:v:1,0,0 dxo:v:1,5 xTe:v:1,1 xTe:v:1,2 sdx:v:1,0,1 xTe:a:1,0
-dTp:v:1,1,1 dTp:v:2,0,1 dTp:v:1,1,0 dwm:v:3,1,0 sdx:v:1,1,1 dwm:v:3,0,0 qx:v:1 dTe:a:2,0,0 qt:v:1,0
-dwm:v:3,0,1 dwm:v:3,1,1 dwo:v:3,0 dTe:v:1,1,1 dTe:v:1,1,0 dwo:a:3,1 dwm:v:2,1,0 dwm:v:0,0,0 dwm:v:0,0,1
-dwo:a:0,0 dwm:v:0,1,0 dwm:v:0,1,1 dwm:v:1,0,0 dwm:v:1,0,1 dwm:v:1,1,0 dwm:v:2,0,0 qt:v:1,1 dwm:v:1,1,1
-dwo:a:0,1 dwo:a:1,0 dwm:v:6,0,0 dwo:a:1,1 dwm:v:2,0,1 dwm:v:2,1,1 dwm:v:5,0,0 dwm:v:5,1,0 sdx:v:1,1,0
-dwm:v:5,1,1 sdw:v:3 dwm:v:6,1,0 dwo:a:2,1 dwm:v:6,0,1 sdw:v:0 dwm:v:5,0,1 dwo:v:2,0 dwm:v:6,1,1 dTp:v:2,1,1
-dTp:v:2,1,0 dwo:v:5,1 dwm:v:4,1,0 dTe:a:2,0,1 dwo:a:5,0 dwo:v:6,0 sdw:v:1 dwo:a:6,1 dwm:v:4,0,0 dwm:v:4,1,1
-sdw:v:2 dwm:v:4,0,1 sdw:v:5 dTe:a:2,1,1 dwm:v:7,1,0 qt:v:2,0 dwm:v:7,1,1 dTe:v:2,1,0 dwm:v:7,0,0 sdw:v:6
-dwo:v:4,1 dwm:v:7,0,1 dwo:a:4,0 dwm:v:9,0,0 qt:v:2,1 sdw:v:4 dwm:v:9,0,1 dwo:a:7,1 dwm:v:9,1,0 dwo:a:7,0
-sdw:v:7 dwo:a:9,0 dwm:v:9,1,1 dwo:v:9,1 sdw:v:9 dwm:v:11,0,0 dwm:v:11,1,0 dwm:v:11,1,1 dwo:a:11,1 dwm:v:11,0,1
-dwo:v:11,0 sdw:v:11 dwm:v:10,1,0 dwm:v:10,1,1 dwo:v:10,1 dwm:v:10,0,0 dwm:v:10,0,1 dwo:v:10,0 sdw:v:10
-dwm:v:8,1,0 dwm:v:8,0,0 dwm:v:8,0,1 dwm:v:8,1,1 dwo:a:8,0 dwo:a:8,1 sdw:v:8
+FLOPS = 2 * 2 * TOKENS * CHANNELS * FEATURES
+BYTES = 2 * (TOKENS * CHANNELS + FEATURES * CHANNELS + BATCH * FEATURES * POOLED) + 4 * (TOKENS + FEATURES) * CHANNELS
+
+ORDER = """
+sort_w:01:S sort_w:00:V quantize_w:00 quantize_w:01
+turn_grads
+copy_grads:0:S copy_grads:1:S copy_grads:2:S copy_grads:3:S copy_grads:4:S copy_grads:5:S
+sort_w:10:V sort_w:11:V quantize_w:10 quantize_w:11
+sort_x:0 turn_x:0 sort_w:20:S copy_x:0:SSSS
+make_dz:10 make_dz:00 quantize_f:10 quantize_f:00 sort_w:21:S make_dz:20 quantize_w:20 quantize_f:20
+turn_dz:10 turn_dz:00 make_dz:01
+dx:00 dx_out:00:SVSS copy_dz:100:S copy_dz:101:S quantize_w:21 make_dz:11
+dx:01 quantize_f:01 dx_out:01:SSSS turn_dz:01 quantize_f:11 make_dz:21 quantize_f:21 copy_dz:011:S
+dx:10 sort_x:1 copy_dz:000:S copy_dz:001:S dx_out:10:SVSS
+dx:11 quantize_t:00 copy_dz:010:V quantize_x:0 dx_out:11:SSVS
+turn_x:1 copy_x:1:VSVS quantize_t:01 quantize_x:1
+turn_dz:11 turn_dz:20 copy_dz:110:S copy_dz:111:S
+dw:00 quantize_t:10 dw:01 dw_out:00:VS copy_dz:201:S quantize_t:11 dw_out:01:VS copy_dz:200:V
+dw:02 dw:03 dw_out:02:VS dw_out:03:VS quantize_t:20
+dw:04 turn_dz:21 dw_out:04:VS dw:05 copy_dz:210:S copy_dz:211:V dw_out:05:VS
+dw:06 quantize_t:21 dw_out:06:VS dw:07 dw_out:07:VS
+dw:08 dw_out:08:VS dw:09 dw_out:09:VS dw:10 dw_out:10:VS dw:11 dw_out:11:VS
 """
 
 
@@ -53,228 +54,225 @@ def tile_pam_module_pa_v_kernel(
     nc = tc.nc
     with ExitStack() as ctx:
         keep = ctx.enter_context(tc.tile_pool(name="keep", bufs=1))
-        work = ctx.enter_context(tc.tile_pool(name="work", bufs=2))
+        work = ctx.enter_context(tc.tile_pool(name="work", bufs=1))
         psum = ctx.enter_context(tc.psum_pool(name="psum", bufs=8))
         ctx.enter_context(tc.manual_schedule())
 
-        gnat = keep.tile([P, 6144], BF16, name="gnat", align_bytes=64)
-        w_raw = [keep.tile([P, 4, C], BF16, name="w_raw%d" % g, align_bytes=64) for g in range(NG)]
-        x_raw = [keep.tile([P, 16, 256], BF16, name="x_raw%d" % h, align_bytes=64) for h in range(2)]
-        ident = keep.tile([P, P], F32, name="ident")
-        make_identity(nc, ident[:])
-        nc.vector.memset(gnat[96:128, :], 0.0)
+        grads = keep.tile([P, PASS * POOLED], BF16, name="grads", align_bytes=64)
+        w_raw = [keep.tile([P, 4, CHANNELS], BF16, name="w_raw%d" % g, align_bytes=64) for g in range(FEATURE_PASSES)]
+        x_raw = [keep.tile([P, PASS_IMAGES, 256], BF16, name="x_raw%d" % h, align_bytes=64) for h in range(TOKEN_PASSES)]
+        identity = keep.tile([P, P], F32, name="identity")
+        warm = keep.tile([P, 2], F32, name="warm")
 
-        rows = "(p j) c -> p j c"
-        grad = "n f v -> n (f v)"
-        half = slice(0, 512), slice(512, 1024)
-        nc.scalar.dma_start(out=gnat[0:32, 0:3072], in_=grad_0.rearrange(grad))
-        nc.scalar.dma_start(out=gnat[0:32, 3072:6144], in_=grad_1.rearrange(grad))
-        nc.sync.dma_start(out=w_raw[1][:, :, half[1]], in_=Wv[0:512, half[1]].rearrange(rows, j=4))
-        nc.sync.dma_start(out=gnat[32:96, :], in_=grad_2.rearrange("n (k f) v -> (n k) (f v)", k=2))
-        nc.sync.dma_start(out=w_raw[1][:, :, half[0]], in_=Wv[0:512, half[0]].rearrange(rows, j=4))
-        nc.sync.dma_start(out=w_raw[2][:], in_=Wv[512:1024, :].rearrange(rows, j=4))
-        nc.sync.dma_start(out=x_raw[0][:], in_=x[0:16].rearrange("n (p e) i j -> p n (e i j)", e=8))
-        nc.sync.dma_start(out=w_raw[0][0:64], in_=Wq.rearrange(rows, j=4))
-        nc.sync.dma_start(out=x_raw[1][:], in_=x[16:32].rearrange("n (p e) i j -> p n (e i j)", e=8))
+        w_view = "(p j) c -> p j c"
+        x_view = "n (p e) i j -> p n (e i j)"
+        nc.sync.dma_start(out=w_raw[0][0:64], in_=Wq.rearrange(w_view, j=4))
+        nc.scalar.dma_start(out=w_raw[0][64:128], in_=Wk.rearrange(w_view, j=4))
+        nc.sync.dma_start(out=grads[32:96, :], in_=grad_2.rearrange("n (k f) v -> (n k) (f v)", k=2))
+        nc.scalar.dma_start(out=grads[0:32, 0 : 256 * POOLED], in_=grad_0.rearrange("n f v -> n (f v)"))
+        nc.scalar.dma_start(out=grads[0:32, 256 * POOLED : 512 * POOLED], in_=grad_1.rearrange("n f v -> n (f v)"))
+        for k in range(2):
+            half = slice(512 * k, 512 * k + 512)
+            nc.sync.dma_start(out=w_raw[1][:, :, half], in_=Wv[0:512, half].rearrange(w_view, j=4))
+        nc.sync.dma_start(out=x_raw[0][:], in_=x[0:16].rearrange(x_view, e=8))
+        nc.sync.dma_start(out=w_raw[2][:], in_=Wv[512:1024, :].rearrange(w_view, j=4))
+        nc.sync.dma_start(out=x_raw[1][:], in_=x[16:32].rearrange(x_view, e=8))
 
-        def lwk(en):
-            nc.scalar.dma_start(out=w_raw[0][64:128], in_=Wk.rearrange(rows, j=4))
+        make_identity(nc, identity[:])
+        nc.vector.memset(grads[GRAD_ROWS:P, :], 0.0)
+        nc.vector.memset(warm[:], 0.0)
+        nc.scalar.activation(out=warm[:, 0:1], in_=warm[:, 1:2], func=COPY)
 
-        g_row = keep.tile([P, 2, 96, 2, 4], BF16, name="g_row", align_bytes=64)
-        g_col = keep.tile([P, 96, 8, 4], BF16, name="g_col", align_bytes=64)
-        w_codes = keep.tile([P, NG, C], U32, name="w_codes", align_bytes=64)
-        w_scales = keep.tile([P, NG, C], U8, name="w_scales", align_bytes=64)
-        f_codes = keep.tile([P, NG, T], U32, name="f_codes", align_bytes=64)
-        f_scales = keep.tile([P, NG, T], U8, name="f_scales", align_bytes=64)
-        t_codes = keep.tile([P, 2, J], U32, name="t_codes", align_bytes=64)
-        t_scales = keep.tile([P, 2, J], U8, name="t_scales", align_bytes=64)
-        x_codes = keep.tile([P, 2, C], U32, name="x_codes", align_bytes=64)
-        x_scales = keep.tile([P, 2, C], U8, name="x_scales", align_bytes=64)
-        tiles = {}
+        row_part = keep.tile([P, GRAD_ROWS, ROWS, 4], BF16, name="row_part", align_bytes=64)
+        col_part = keep.tile([P, GRAD_ROWS, COLS, 4], BF16, name="col_part", align_bytes=64)
 
-        def bank(key, shape, dtype=F32):
-            b = psum.tile(shape, dtype, name="bank", tag="bank", bufs=8)
-            tiles[key] = b
-            return b
+        def operand(name, passes, width):
+            codes = keep.tile([P, passes, width], U32, name=name + "_codes", align_bytes=64)
+            scales = keep.tile([P, passes, width], U8, name=name + "_scales", align_bytes=64)
+            return codes, scales
 
-        def stage(key, tag, bufs):
-            t = work.tile([P, 4096 if tag[0] == "x" else 2048], BF16, name=tag, tag=tag, bufs=bufs, align_bytes=64)
-            tiles[key] = t
-            return t
+        w_q = operand("w", FEATURE_PASSES, CHANNELS)
+        f_q = operand("f", FEATURE_PASSES, TOKENS)
+        t_q = operand("t", TOKEN_PASSES, FEATURES)
+        x_q = operand("x", TOKEN_PASSES, CHANNELS)
+
+        def quantize(quantized, fmt, index, cols, source):
+            codes, scales = quantized
+            nc.vector.quantize_mx(out=codes[:, index, cols].bitcast(fmt), scales=scales[:, index, cols], in_=source[:])
+
+        def multiply(out, weights, w_fmt, w_cols, moving, m_fmt, m_cols, index, passes):
+            nc.tensor.matmul_mx(
+                out=out[:],
+                lhsT=weights[0][:, index, w_cols].bitcast(w_fmt),
+                lhsT_scale=weights[1][:, index, w_cols],
+                rhs=moving[0][:, index, m_cols].bitcast(m_fmt),
+                rhs_scale=moving[1][:, index, m_cols],
+                start=(index == 0),
+                stop=(index == passes - 1),
+            )
 
         def move(engine, out, in_):
-            if engine == "a":
+            if engine == "S":
                 nc.scalar.copy(out=out, in_=in_)
             else:
                 nc.vector.tensor_copy(out=out, in_=in_)
 
-        g_words = gnat[:].bitcast(F32).rearrange("q (m t w) -> q t w m", t=4, w=6)
+        tiles = {}
 
-        def gTp(en, w):
-            pg = bank(("g", w), [P, 4, P])
-            for t in range(4):
-                nc.tensor.transpose(pg[:, t, :], g_words[:, t, w, :], ident[:])
+        def bank(*key):
+            tiles[key] = psum.tile([P, BANK], F32, name="bank", tag="bank", bufs=8)
+            return tiles[key]
 
-        def gTe(en, w):
-            src = tiles["g", w][:].rearrange("p t q -> p (t q)").bitcast(BF16)
-            src = src.rearrange("p (t q a) -> p q a t", t=4, a=2)
-            if w < 2:
-                out, factor = g_row[:, w], 0.125
+        def stage(tag, bufs, width, *key):
+            tiles[key] = work.tile([P, width], BF16, name=tag, tag=tag, bufs=bufs, align_bytes=64)
+            return tiles[key]
+
+        grad_words = grads[:].bitcast(F32).rearrange("q (p t w) -> w t q p", t=4, w=POOLED // 2)
+
+        def turn_grads():
+            for w in range(POOLED // 2):
+                out = bank("grads", w)
+                for t in range(4):
+                    nc.tensor.transpose(out[:, P * t : P * t + P], grad_words[w, t], identity[:])
+
+        def copy_grads(w, engines):
+            words = tiles["grads", w][:].bitcast(BF16).rearrange("p (t q a) -> p q a t", t=4, a=2)
+            if 2 * w < ROWS:
+                out, factor = row_part[:, :, 2 * w : 2 * w + 2, :], 1.0 / COLS
             else:
-                out, factor = g_col[:, :, 2 * (w - 2) : 2 * (w - 2) + 2, :], 0.25
-            halves = (
-                (out[:, 0:32], src[:, 0:32]),
-                (
-                    out[:, 32:96].rearrange("p (k n) a t -> p n k a t", k=2),
-                    src[:, 32:96].rearrange("p (n k) a t -> p n k a t", k=2),
-                ),
+                out, factor = col_part[:, :, 2 * w - ROWS : 2 * w - ROWS + 2, :], 1.0 / ROWS
+            first = (out[:, 0:BATCH], words[:, 0:BATCH])
+            others = (
+                out[:, BATCH:GRAD_ROWS].rearrange("p (k n) a t -> p n k a t", k=2),
+                words[:, BATCH:GRAD_ROWS].rearrange("p (n k) a t -> p n k a t", k=2),
             )
-            for dst, part in halves:
-                if en == "a":
-                    nc.scalar.activation(out=dst, in_=part, func=COPY, scale=factor)
+            for dst, src in (first, others):
+                if engines == "S":
+                    nc.scalar.activation(out=dst, in_=src, func=COPY, scale=factor)
                 else:
-                    nc.vector.tensor_scalar_mul(dst, part, factor)
+                    nc.vector.tensor_scalar_mul(dst, src, factor)
 
-        def add(en, g, h):
-            dz = stage(("dz", g, h), "dz", 4)
-            q0 = 32 * g + 16 * h
-            row_shape, col_shape = [P, 32, 8, 4], [P, 16, 2, 32]
-            col = g_col[:, q0 : q0 + 16].rearrange("p n j t -> p n (j t)").unsqueeze(2).to_broadcast(col_shape)
-            for u in range(2):
-                row = g_row[:, u, q0 : q0 + 16].rearrange("p n a t -> p (n a) t")
+        def make_dz(g, h):
+            dz = stage("dz", 4, 4 * PASS, "dz", g, h)
+            images = slice(BATCH * g + PASS_IMAGES * h, BATCH * g + PASS_IMAGES * (h + 1))
+            row = row_part[:, images].rearrange("p m i t -> p m (i t)").unsqueeze(2)
+            col = col_part[:, images].rearrange("p m (k s) t -> p s (m k) t", k=2)
+            for s in range(4):
                 nc.vector.tensor_tensor(
-                    out=dz[:, 1024 * u : 1024 * (u + 1)].rearrange("p (e q t) -> p q e t", e=2, t=4),
-                    in0=row.unsqueeze(2).to_broadcast(row_shape),
-                    in1=col,
+                    out=dz[:, PASS * s : PASS * s + PASS],
+                    in0=row.to_broadcast([P, PASS_IMAGES, 2, 4 * ROWS]),
+                    in1=col[:, s].unsqueeze(2).to_broadcast([P, 2 * PASS_IMAGES, ROWS, 4]),
                     op=ADD,
                 )
 
-        def qf(en, g, h):
-            cols = slice(512 * h, 512 * h + 512)
-            nc.vector.quantize_mx(
-                out=f_codes[:, g, cols].bitcast(E5M2), scales=f_scales[:, g, cols], in_=tiles["dz", g, h][:]
-            )
+        def quantize_f(g, h):
+            quantize(f_q, E5M2, g, slice(PASS * h, PASS * h + PASS), tiles["dz", g, h])
 
-        def dTp(en, g, h, v):
-            words = tiles["dz", g, h][:].bitcast(F32).rearrange("p (s q v) -> p s q v", s=4, v=2)
-            pt = bank(("d", g, h, v), [P, 4, P])
-            for s in range(4):
-                nc.tensor.transpose(pt[:, s, :], words[:, s, :, v], ident[:])
+        def turn_dz(g, h):
+            words = tiles["dz", g, h][:].bitcast(F32).rearrange("p (s q v) -> v s p q", s=4, v=2)
+            for v in range(2):
+                out = bank("dz", g, h, v)
+                for s in range(4):
+                    nc.tensor.transpose(out[:, P * s : P * s + P], words[v, s], identity[:])
 
-        def dTe(en, g, h, v):
+        def copy_dz(g, h, v, engines):
             if ("tok", g, h) not in tiles:
-                stage(("tok", g, h), "tok", 3)
-            dst = tiles["tok", g, h][:].rearrange("q (p v f s) -> q v p f s", v=2, f=2, s=4)
-            src = tiles["d", g, h, v][:].rearrange("q s p -> q (s p)").bitcast(BF16)
-            move(en, dst[:, v], src.rearrange("q (s p f) -> q p f s", s=4, f=2))
+                stage("tok", 3, 4 * PASS, "tok", g, h)
+            dst = tiles["tok", g, h][:].rearrange("q (p v fs) -> v q p fs", v=2, fs=8)
+            src = tiles["dz", g, h, v][:].bitcast(BF16).rearrange("q (s p f) -> q p f s", s=4, f=2)
+            move(engines, dst[v].rearrange("q p (f s) -> q p f s", f=2), src)
 
-        def qt(en, g, h):
-            cols = slice(512 * g, 512 * g + 512)
-            nc.vector.quantize_mx(
-                out=t_codes[:, h, cols].bitcast(E5M2), scales=t_scales[:, h, cols], in_=tiles["tok", g, h][:]
-            )
+        def quantize_t(g, h):
+            quantize(t_q, E5M2, h, slice(PASS * g, PASS * g + PASS), tiles["tok", g, h])
 
-        def wc(en, g, k):
-            grouped = stage(("wg", g, k), "wg", 3)
+        def sort_w(g, k, engines):
+            out = stage("w", 3, 4 * 512, "w", g, k)
             move(
-                en,
-                grouped[:].rearrange("p (e m j) -> p e m j", e=4, j=4),
+                engines,
+                out[:].rearrange("p (e m j) -> p e m j", e=4, j=4),
                 w_raw[g][:, :, 512 * k : 512 * k + 512].rearrange("p j (m e) -> p e m j", e=4),
             )
 
-        def qw(en, g, k):
-            cols = slice(512 * k, 512 * k + 512)
-            nc.vector.quantize_mx(
-                out=w_codes[:, g, cols].bitcast(E4M3), scales=w_scales[:, g, cols], in_=tiles["wg", g, k][:]
-            )
+        def quantize_w(g, k):
+            quantize(w_q, E4M3, g, slice(512 * k, 512 * k + 512), tiles["w", g, k])
 
-        def xs(en, h):
-            xr = stage(("xr", h), "xr", 1)
-            move(
-                en,
-                xr[:].rearrange("p (b n k) -> p b n k", b=16, n=16),
-                x_raw[h][:].rearrange("p n (b k) -> p b n k", k=16),
-            )
+        def sort_x(h):
+            out = stage("x_sorted", 1, 256 * PASS_IMAGES, "x_sorted", h)
+            dst = out[:].bitcast(F32).rearrange("p (e u m k i) -> p u e m k i", e=8, u=2, m=PASS_IMAGES, k=2)
+            src = x_raw[h][:].bitcast(F32).rearrange("p m (e i k u) -> p u e m k i", e=8, i=ROWS, k=2)
+            for u in range(2):
+                nc.vector.tensor_copy(out=dst[:, u], in_=src[:, u])
 
-        def xTp(en, h, k):
-            words = tiles["xr", h][:].bitcast(F32).rearrange("p (b q) -> p b q", b=16)
-            px = bank(("x", h, k), [P, 4, P])
-            for s in range(4):
-                nc.tensor.transpose(px[:, s, :], words[:, 4 * k + s, :], ident[:])
+        def turn_x(h):
+            words = tiles["x_sorted", h][:].bitcast(F32)
+            for b in range(4):
+                out = bank("x", h, b)
+                for r in range(4):
+                    run = slice(P * (4 * b + r), P * (4 * b + r) + P)
+                    nc.tensor.transpose(out[:, P * r : P * r + P], words[:, run], identity[:])
 
-        def xTe(en, h, k):
-            if ("xg", h) not in tiles:
-                stage(("xg", h), "xg", 1)
-            dst = tiles["xg", h][:].bitcast(F32).rearrange("q (p s) -> q p s", s=16)[:, :, 4 * k : 4 * k + 4]
-            move(en, dst, tiles["x", h, k][:].rearrange("q s p -> q p s"))
+        def copy_x(h, engines):
+            out = stage("x", 1, 4 * CHANNELS, "x", h)
+            dst = out[:].bitcast(F32).rearrange("q (p b r) -> b q p r", b=4, r=4)
+            for b in range(4):
+                move(engines[b], dst[b], tiles["x", h, b][:].rearrange("q (r p) -> q p r", r=4))
 
-        def qx(en, h):
-            nc.vector.quantize_mx(
-                out=x_codes[:, h, :].bitcast(E4M3), scales=x_scales[:, h, :], in_=tiles["xg", h][:]
-            )
+        def quantize_x(h):
+            quantize(x_q, E4M3, h, slice(0, CHANNELS), tiles["x", h])
 
-        def dxm(en, h, e, g):
-            acc = bank(("dx", h, e), [P, 512]) if g == 0 else tiles["dx", h, e]
-            wcol = slice(128 * e, 128 * e + 128)
-            tk = slice(512 * h, 512 * h + 512)
-            nc.tensor.matmul_mx(
-                out=acc[:],
-                lhsT=w_codes[:, g, wcol].bitcast(E4M3),
-                lhsT_scale=w_scales[:, g, wcol],
-                rhs=f_codes[:, g, tk].bitcast(E5M2),
-                rhs_scale=f_scales[:, g, tk],
-                start=(g == 0),
-                stop=(g == NG - 1),
-            )
+        def dx(h, k):
+            for e in range(4):
+                bank("dx", h, k, e)
+            for g in range(FEATURE_PASSES):
+                for e in range(4):
+                    channels = slice(512 * k + P * e, 512 * k + P * e + P)
+                    tokens = slice(PASS * h, PASS * h + PASS)
+                    multiply(tiles["dx", h, k, e], w_q, E4M3, channels, f_q, E5M2, tokens, g, FEATURE_PASSES)
 
-        def dxo(en, h, e):
-            k = e // 4
-            if ("dxt", h, k) not in tiles:
-                tiles["dxt", h, k] = work.tile([P, 16, 4, 32], F32, name="dx_out", tag="dx_out", bufs=4)
-            dst = tiles["dxt", h, k][:, :, e % 4, :].rearrange("m n (u k e) -> m u n k e", u=2, e=2)
-            move(en, dst, tiles["dx", h, e][:].rearrange("m (u e n k) -> m u n k e", u=2, e=2, n=16))
+        def dx_out(h, k, engines):
+            out = work.tile([P, PASS_IMAGES, 4, ROWS * COLS], F32, name="dx_rows", tag="dx_rows", bufs=4)
+            for e in range(4):
+                dst = out[:, :, e, :].rearrange("c m (i k s) -> c m k i s", i=ROWS, k=2)
+                move(engines[e], dst, tiles["dx", h, k, e][:].rearrange("c (s m k i) -> c m k i s", s=4, k=2, i=ROWS))
+            for b in range(2):
+                n0 = PASS_IMAGES * h + 8 * b
+                nc.sync.dma_start(
+                    out=out_0[n0 : n0 + 8, 512 * k : 512 * k + 512].rearrange("n (m e) i j -> m n (e i j)", e=4),
+                    in_=out[:, 8 * b : 8 * b + 8].rearrange("c m e t -> c m (e t)"),
+                )
 
-        def sdx(en, h, k, i):
-            n0 = 16 * h + 8 * i
-            nc.sync.dma_start(
-                out=out_0[n0 : n0 + 8, 512 * k : 512 * k + 512].rearrange("n (m e) i j -> m n (e i j)", e=4),
-                in_=tiles["dxt", h, k][:, 8 * i : 8 * i + 8].rearrange("m n e t -> m n (e t)"),
-            )
+        def dw(block):
+            features = slice(P * block, P * block + P)
+            for b in range(2):
+                out = bank("dw", block, b)
+                for h in range(TOKEN_PASSES):
+                    channels = slice(BANK * b, BANK * b + BANK)
+                    multiply(out, t_q, E5M2, features, x_q, E4M3, channels, h, TOKEN_PASSES)
 
-        def dwm(en, oc, b, h):
-            acc = bank(("dw", oc, b), [P, 512]) if h == 0 else tiles["dw", oc, b]
-            fc = slice(128 * oc, 128 * oc + 128)
-            cc = slice(512 * b, 512 * b + 512)
-            nc.tensor.matmul_mx(
-                out=acc[:],
-                lhsT=t_codes[:, h, fc].bitcast(E5M2),
-                lhsT_scale=t_scales[:, h, fc],
-                rhs=x_codes[:, h, cc].bitcast(E4M3),
-                rhs_scale=x_scales[:, h, cc],
-                start=(h == 0),
-                stop=(h == 1),
-            )
-
-        def dwo(en, oc, b):
-            if ("row", oc) not in tiles:
-                tiles["row", oc] = work.tile([P, C], F32, name="dw_out", tag="dw_out", bufs=4)
-            move(en, tiles["row", oc][:, 512 * b : 512 * b + 512], tiles["dw", oc, b][:])
-
-        def sdw(en, oc):
-            fc = slice(128 * oc, 128 * oc + 128)
-            if oc < 2:
-                dst = out_1[fc, :]
-            elif oc < 4:
-                dst = out_2[128 * (oc - 2) : 128 * (oc - 1), :]
+        def dw_out(block, engines):
+            out = work.tile([P, CHANNELS], F32, name="dw_rows", tag="dw_rows", bufs=4)
+            for b in range(2):
+                move(engines[b], out[:, BANK * b : BANK * b + BANK], tiles["dw", block, b][:])
+            f0 = P * block
+            if f0 < 256:
+                dst = out_1[f0 : f0 + P, :]
+            elif f0 < 512:
+                dst = out_2[f0 - 256 : f0 - 256 + P, :]
             else:
-                dst = out_3[128 * (oc - 4) : 128 * (oc - 3), :]
-            nc.sync.dma_start(out=dst, in_=tiles["row", oc][:])
+                dst = out_3[f0 - 512 : f0 - 512 + P, :]
+            nc.sync.dma_start(out=dst, in_=out[:])
 
         steps = {
-            "gTp": gTp, "gTe": gTe, "add": add, "qf": qf, "dTp": dTp, "dTe": dTe, "qt": qt, "wc": wc, "qw": qw,
-            "lwk": lwk, "xs": xs, "xTp": xTp, "xTe": xTe, "qx": qx, "dxm": dxm, "dxo": dxo, "sdx": sdx, "dwm": dwm, "dwo": dwo,
-            "sdw": sdw,
+            "turn_grads": turn_grads, "copy_grads": copy_grads, "make_dz": make_dz, "quantize_f": quantize_f,
+            "turn_dz": turn_dz, "copy_dz": copy_dz, "quantize_t": quantize_t, "sort_w": sort_w, "quantize_w": quantize_w,
+            "sort_x": sort_x, "turn_x": turn_x, "copy_x": copy_x, "quantize_x": quantize_x, "dx": dx, "dx_out": dx_out,
+            "dw": dw, "dw_out": dw_out,
         }
-        for step in PLAN.split():
-            name, engine, where = step.split(":")
-            steps[name](engine, *[int(i) for i in where.split(",") if i])
+        for entry in ORDER.split():
+            name, *rest = entry.split(":")
+            where = rest[:1]
+            if name in ("dw", "dw_out"):
+                numbers = [int(digits) for digits in where]
+            else:
+                numbers = [int(digit) for digits in where for digit in digits]
+            steps[name](*numbers, *rest[1:])

from contextlib import ExitStack

import concourse.mybir as mybir
from concourse.masks import make_identity

F32 = mybir.dt.float32
BF16 = mybir.dt.bfloat16
U32 = mybir.dt.uint32
U8 = mybir.dt.uint8
E4M3 = mybir.dt.float8_e4m3fn_x4
E5M2 = mybir.dt.float8_e5m2_x4
COPY = mybir.ActivationFunctionType.Copy
ADD = mybir.AluOpType.add

P = 128
BATCH, ROWS, COLS = 32, 4, 8
TOKENS, CHANNELS, FEATURES = BATCH * ROWS * COLS, 1024, 1536
PASS = 512
FEATURE_PASSES = FEATURES // PASS
TOKEN_PASSES = TOKENS // PASS
PASS_IMAGES = BATCH // TOKEN_PASSES
POOLED = ROWS + COLS
GRAD_ROWS = FEATURE_PASSES * BATCH
BANK = 512

FLOPS = 2 * 2 * TOKENS * CHANNELS * FEATURES
BYTES = 2 * (TOKENS * CHANNELS + FEATURES * CHANNELS + BATCH * FEATURES * POOLED) + 4 * (TOKENS + FEATURES) * CHANNELS

ORDER = """
sort_w:01:S sort_w:00:V quantize_w:00 quantize_w:01
turn_grads
copy_grads:0:S copy_grads:1:S copy_grads:2:S copy_grads:3:S copy_grads:4:S copy_grads:5:S
sort_w:10:V sort_w:11:V quantize_w:10 quantize_w:11
sort_x:0 turn_x:0 sort_w:20:S copy_x:0:SSSS
make_dz:10 make_dz:00 quantize_f:10 quantize_f:00 sort_w:21:S make_dz:20 quantize_w:20 quantize_f:20
turn_dz:10 turn_dz:00 make_dz:01
dx:00 dx_out:00:SVSS copy_dz:100:S copy_dz:101:S quantize_w:21 make_dz:11
dx:01 quantize_f:01 dx_out:01:SSSS turn_dz:01 quantize_f:11 make_dz:21 quantize_f:21 copy_dz:011:S
dx:10 sort_x:1 copy_dz:000:S copy_dz:001:S dx_out:10:SVSS
dx:11 quantize_t:00 copy_dz:010:V quantize_x:0 dx_out:11:SSVS
turn_x:1 copy_x:1:VSVS quantize_t:01 quantize_x:1
turn_dz:11 turn_dz:20 copy_dz:110:S copy_dz:111:S
dw:00 quantize_t:10 dw:01 dw_out:00:VS copy_dz:201:S quantize_t:11 dw_out:01:VS copy_dz:200:V
dw:02 dw:03 dw_out:02:VS dw_out:03:VS quantize_t:20
dw:04 turn_dz:21 dw_out:04:VS dw:05 copy_dz:210:S copy_dz:211:V dw_out:05:VS
dw:06 quantize_t:21 dw_out:06:VS dw:07 dw_out:07:VS
dw:08 dw_out:08:VS dw:09 dw_out:09:VS dw:10 dw_out:10:VS dw:11 dw_out:11:VS
"""


def tile_pam_module_pa_v_kernel(
    tc, x, Wq, bq, Wk, bk, Wv, bv, grad_0, grad_1, grad_2, out_0, out_1, out_2, out_3
):
    nc = tc.nc
    with ExitStack() as ctx:
        keep = ctx.enter_context(tc.tile_pool(name="keep", bufs=1))
        work = ctx.enter_context(tc.tile_pool(name="work", bufs=1))
        psum = ctx.enter_context(tc.psum_pool(name="psum", bufs=8))
        ctx.enter_context(tc.manual_schedule())

        grads = keep.tile([P, PASS * POOLED], BF16, name="grads", align_bytes=64)
        w_raw = [keep.tile([P, 4, CHANNELS], BF16, name="w_raw%d" % g, align_bytes=64) for g in range(FEATURE_PASSES)]
        x_raw = [keep.tile([P, PASS_IMAGES, 256], BF16, name="x_raw%d" % h, align_bytes=64) for h in range(TOKEN_PASSES)]
        identity = keep.tile([P, P], F32, name="identity")
        warm = keep.tile([P, 2], F32, name="warm")

        w_view = "(p j) c -> p j c"
        x_view = "n (p e) i j -> p n (e i j)"
        nc.sync.dma_start(out=w_raw[0][0:64], in_=Wq.rearrange(w_view, j=4))
        nc.scalar.dma_start(out=w_raw[0][64:128], in_=Wk.rearrange(w_view, j=4))
        nc.sync.dma_start(out=grads[32:96, :], in_=grad_2.rearrange("n (k f) v -> (n k) (f v)", k=2))
        nc.scalar.dma_start(out=grads[0:32, 0 : 256 * POOLED], in_=grad_0.rearrange("n f v -> n (f v)"))
        nc.scalar.dma_start(out=grads[0:32, 256 * POOLED : 512 * POOLED], in_=grad_1.rearrange("n f v -> n (f v)"))
        for k in range(2):
            half = slice(512 * k, 512 * k + 512)
            nc.sync.dma_start(out=w_raw[1][:, :, half], in_=Wv[0:512, half].rearrange(w_view, j=4))
        nc.sync.dma_start(out=x_raw[0][:], in_=x[0:16].rearrange(x_view, e=8))
        nc.sync.dma_start(out=w_raw[2][:], in_=Wv[512:1024, :].rearrange(w_view, j=4))
        nc.sync.dma_start(out=x_raw[1][:], in_=x[16:32].rearrange(x_view, e=8))

        make_identity(nc, identity[:])
        nc.vector.memset(grads[GRAD_ROWS:P, :], 0.0)
        nc.vector.memset(warm[:], 0.0)
        nc.scalar.activation(out=warm[:, 0:1], in_=warm[:, 1:2], func=COPY)

        row_part = keep.tile([P, GRAD_ROWS, ROWS, 4], BF16, name="row_part", align_bytes=64)
        col_part = keep.tile([P, GRAD_ROWS, COLS, 4], BF16, name="col_part", align_bytes=64)

        def operand(name, passes, width):
            codes = keep.tile([P, passes, width], U32, name=name + "_codes", align_bytes=64)
            scales = keep.tile([P, passes, width], U8, name=name + "_scales", align_bytes=64)
            return codes, scales

        w_q = operand("w", FEATURE_PASSES, CHANNELS)
        f_q = operand("f", FEATURE_PASSES, TOKENS)
        t_q = operand("t", TOKEN_PASSES, FEATURES)
        x_q = operand("x", TOKEN_PASSES, CHANNELS)

        def quantize(quantized, fmt, index, cols, source):
            codes, scales = quantized
            nc.vector.quantize_mx(out=codes[:, index, cols].bitcast(fmt), scales=scales[:, index, cols], in_=source[:])

        def multiply(out, weights, w_fmt, w_cols, moving, m_fmt, m_cols, index, passes):
            nc.tensor.matmul_mx(
                out=out[:],
                lhsT=weights[0][:, index, w_cols].bitcast(w_fmt),
                lhsT_scale=weights[1][:, index, w_cols],
                rhs=moving[0][:, index, m_cols].bitcast(m_fmt),
                rhs_scale=moving[1][:, index, m_cols],
                start=(index == 0),
                stop=(index == passes - 1),
            )

        def move(engine, out, in_):
            if engine == "S":
                nc.scalar.copy(out=out, in_=in_)
            else:
                nc.vector.tensor_copy(out=out, in_=in_)

        tiles = {}

        def bank(*key):
            tiles[key] = psum.tile([P, BANK], F32, name="bank", tag="bank", bufs=8)
            return tiles[key]

        def stage(tag, bufs, width, *key):
            tiles[key] = work.tile([P, width], BF16, name=tag, tag=tag, bufs=bufs, align_bytes=64)
            return tiles[key]

        grad_words = grads[:].bitcast(F32).rearrange("q (p t w) -> w t q p", t=4, w=POOLED // 2)

        def turn_grads():
            for w in range(POOLED // 2):
                out = bank("grads", w)
                for t in range(4):
                    nc.tensor.transpose(out[:, P * t : P * t + P], grad_words[w, t], identity[:])

        def copy_grads(w, engines):
            words = tiles["grads", w][:].bitcast(BF16).rearrange("p (t q a) -> p q a t", t=4, a=2)
            if 2 * w < ROWS:
                out, factor = row_part[:, :, 2 * w : 2 * w + 2, :], 1.0 / COLS
            else:
                out, factor = col_part[:, :, 2 * w - ROWS : 2 * w - ROWS + 2, :], 1.0 / ROWS
            first = (out[:, 0:BATCH], words[:, 0:BATCH])
            others = (
                out[:, BATCH:GRAD_ROWS].rearrange("p (k n) a t -> p n k a t", k=2),
                words[:, BATCH:GRAD_ROWS].rearrange("p (n k) a t -> p n k a t", k=2),
            )
            for dst, src in (first, others):
                if engines == "S":
                    nc.scalar.activation(out=dst, in_=src, func=COPY, scale=factor)
                else:
                    nc.vector.tensor_scalar_mul(dst, src, factor)

        def make_dz(g, h):
            dz = stage("dz", 4, 4 * PASS, "dz", g, h)
            images = slice(BATCH * g + PASS_IMAGES * h, BATCH * g + PASS_IMAGES * (h + 1))
            row = row_part[:, images].rearrange("p m i t -> p m (i t)").unsqueeze(2)
            col = col_part[:, images].rearrange("p m (k s) t -> p s (m k) t", k=2)
            for s in range(4):
                nc.vector.tensor_tensor(
                    out=dz[:, PASS * s : PASS * s + PASS],
                    in0=row.to_broadcast([P, PASS_IMAGES, 2, 4 * ROWS]),
                    in1=col[:, s].unsqueeze(2).to_broadcast([P, 2 * PASS_IMAGES, ROWS, 4]),
                    op=ADD,
                )

        def quantize_f(g, h):
            quantize(f_q, E5M2, g, slice(PASS * h, PASS * h + PASS), tiles["dz", g, h])

        def turn_dz(g, h):
            words = tiles["dz", g, h][:].bitcast(F32).rearrange("p (s q v) -> v s p q", s=4, v=2)
            for v in range(2):
                out = bank("dz", g, h, v)
                for s in range(4):
                    nc.tensor.transpose(out[:, P * s : P * s + P], words[v, s], identity[:])

        def copy_dz(g, h, v, engines):
            if ("tok", g, h) not in tiles:
                stage("tok", 3, 4 * PASS, "tok", g, h)
            dst = tiles["tok", g, h][:].rearrange("q (p v fs) -> v q p fs", v=2, fs=8)
            src = tiles["dz", g, h, v][:].bitcast(BF16).rearrange("q (s p f) -> q p f s", s=4, f=2)
            move(engines, dst[v].rearrange("q p (f s) -> q p f s", f=2), src)

        def quantize_t(g, h):
            quantize(t_q, E5M2, h, slice(PASS * g, PASS * g + PASS), tiles["tok", g, h])

        def sort_w(g, k, engines):
            out = stage("w", 3, 4 * 512, "w", g, k)
            move(
                engines,
                out[:].rearrange("p (e m j) -> p e m j", e=4, j=4),
                w_raw[g][:, :, 512 * k : 512 * k + 512].rearrange("p j (m e) -> p e m j", e=4),
            )

        def quantize_w(g, k):
            quantize(w_q, E4M3, g, slice(512 * k, 512 * k + 512), tiles["w", g, k])

        def sort_x(h):
            out = stage("x_sorted", 1, 256 * PASS_IMAGES, "x_sorted", h)
            dst = out[:].bitcast(F32).rearrange("p (e u m k i) -> p u e m k i", e=8, u=2, m=PASS_IMAGES, k=2)
            src = x_raw[h][:].bitcast(F32).rearrange("p m (e i k u) -> p u e m k i", e=8, i=ROWS, k=2)
            for u in range(2):
                nc.vector.tensor_copy(out=dst[:, u], in_=src[:, u])

        def turn_x(h):
            words = tiles["x_sorted", h][:].bitcast(F32)
            for b in range(4):
                out = bank("x", h, b)
                for r in range(4):
                    run = slice(P * (4 * b + r), P * (4 * b + r) + P)
                    nc.tensor.transpose(out[:, P * r : P * r + P], words[:, run], identity[:])

        def copy_x(h, engines):
            out = stage("x", 1, 4 * CHANNELS, "x", h)
            dst = out[:].bitcast(F32).rearrange("q (p b r) -> b q p r", b=4, r=4)
            for b in range(4):
                move(engines[b], dst[b], tiles["x", h, b][:].rearrange("q (r p) -> q p r", r=4))

        def quantize_x(h):
            quantize(x_q, E4M3, h, slice(0, CHANNELS), tiles["x", h])

        def dx(h, k):
            for e in range(4):
                bank("dx", h, k, e)
            for g in range(FEATURE_PASSES):
                for e in range(4):
                    channels = slice(512 * k + P * e, 512 * k + P * e + P)
                    tokens = slice(PASS * h, PASS * h + PASS)
                    multiply(tiles["dx", h, k, e], w_q, E4M3, channels, f_q, E5M2, tokens, g, FEATURE_PASSES)

        def dx_out(h, k, engines):
            out = work.tile([P, PASS_IMAGES, 4, ROWS * COLS], F32, name="dx_rows", tag="dx_rows", bufs=4)
            for e in range(4):
                dst = out[:, :, e, :].rearrange("c m (i k s) -> c m k i s", i=ROWS, k=2)
                move(engines[e], dst, tiles["dx", h, k, e][:].rearrange("c (s m k i) -> c m k i s", s=4, k=2, i=ROWS))
            for b in range(2):
                n0 = PASS_IMAGES * h + 8 * b
                nc.sync.dma_start(
                    out=out_0[n0 : n0 + 8, 512 * k : 512 * k + 512].rearrange("n (m e) i j -> m n (e i j)", e=4),
                    in_=out[:, 8 * b : 8 * b + 8].rearrange("c m e t -> c m (e t)"),
                )

        def dw(block):
            features = slice(P * block, P * block + P)
            for b in range(2):
                out = bank("dw", block, b)
                for h in range(TOKEN_PASSES):
                    channels = slice(BANK * b, BANK * b + BANK)
                    multiply(out, t_q, E5M2, features, x_q, E4M3, channels, h, TOKEN_PASSES)

        def dw_out(block, engines):
            out = work.tile([P, CHANNELS], F32, name="dw_rows", tag="dw_rows", bufs=4)
            for b in range(2):
                move(engines[b], out[:, BANK * b : BANK * b + BANK], tiles["dw", block, b][:])
            f0 = P * block
            if f0 < 256:
                dst = out_1[f0 : f0 + P, :]
            elif f0 < 512:
                dst = out_2[f0 - 256 : f0 - 256 + P, :]
            else:
                dst = out_3[f0 - 512 : f0 - 512 + P, :]
            nc.sync.dma_start(out=dst, in_=out[:])

        steps = {
            "turn_grads": turn_grads, "copy_grads": copy_grads, "make_dz": make_dz, "quantize_f": quantize_f,
            "turn_dz": turn_dz, "copy_dz": copy_dz, "quantize_t": quantize_t, "sort_w": sort_w, "quantize_w": quantize_w,
            "sort_x": sort_x, "turn_x": turn_x, "copy_x": copy_x, "quantize_x": quantize_x, "dx": dx, "dx_out": dx_out,
            "dw": dw, "dw_out": dw_out,
        }
        for entry in ORDER.split():
            name, *rest = entry.split(":")
            where = rest[:1]
            if name in ("dw", "dw_out"):
                numbers = [int(digits) for digits in where]
            else:
                numbers = [int(digit) for digits in where for digit in digits]
            steps[name](*numbers, *rest[1:])
